import numpy as np
import ml_dtypes


def mxq(x, axis, fmt="e4m3"):
    dtype, down = {"e4m3": (ml_dtypes.float8_e4m3fn, 7), "e5m2": (ml_dtypes.float8_e5m2, 14)}[fmt]
    v = np.moveaxis(np.asarray(x, np.float32).astype(ml_dtypes.bfloat16).astype(np.float64), axis, -1)
    blocks = v.reshape(v.shape[:-1] + (-1, 32))
    amax = np.abs(blocks).max(-1, keepdims=True)
    byte = np.maximum(np.where(amax > 0, np.frexp(amax)[1] - 1 + 127, 0) - down, 1)
    scale = np.exp2(byte - 127.0)
    codes = (blocks / scale).astype(np.float32).astype(dtype).astype(np.float64)
    return np.moveaxis((codes * scale).reshape(v.shape), -1, axis)


BF16 = ml_dtypes.bfloat16


def bf(x):
    return np.asarray(x, np.float32).astype(BF16)


def f64(x):
    return np.asarray(x).astype(np.float64)


B, D, C, R = 8192, 512, 128, 8

C_CURV = 1.0
EPS = 1e-15
PROJ_EPS = 1e-5


def clamp_abs(v, eps=EPS):
    return np.maximum(np.abs(v), eps) * np.sign(v)


def arcsinh(v):
    return np.sign(v) * np.log(np.abs(v) + np.sqrt(v * v + 1.0))


def draw_rows(n, u, lo, hi):
    z = np.random.standard_normal((n, R)) / np.sqrt(R)
    v = 0.5 * np.random.standard_normal((n, D)) / np.sqrt(D)
    for i in range(R):
        v = v + z[:, i:i + 1] * u[i]
    return v / np.sqrt(np.sum(v * v, axis=1, keepdims=True)) * np.random.uniform(lo, hi, (n, 1))


def setup_inputs():
    u = np.random.standard_normal((R, D)) / np.sqrt(D)
    return {"x": bf(draw_rows(B, u, 0.4, 1.6)), "a": bf(draw_rows(C, u, 0.5, 2.0)), "p": bf(draw_rows(C, u, 0.3, 0.9))}


def reference(x, a, p):
    x, a, p = f64(x), f64(a), f64(p)
    k = C_CURV
    sqrt_k = np.sqrt(k)

    xn = np.maximum(np.sqrt(np.sum(x * x, axis=-1, keepdims=True)), EPS)
    maxn = (1.0 - PROJ_EPS) / sqrt_k
    x = np.where(xn > maxn, x * (maxn / xn), x)

    x2 = np.sum(x * x, axis=-1)
    p2 = np.sum(p * p, axis=-1)
    xq = mxq(x, 1, "e4m3")
    px = xq @ mxq(p, 1, "e4m3").T
    xa = xq @ mxq(a, 1, "e4m3").T
    pa = np.sum(p * a, axis=-1)
    a_norm = np.sqrt(np.sum(a * a, axis=-1))

    A = 1.0 - 2.0 * k * px + k * x2[:, None]
    Bc = 1.0 - k * p2
    den = np.maximum(1.0 - 2.0 * k * px + (k * k) * x2[:, None] * p2[None, :], EPS)

    diff_norm2 = np.maximum(
        (A * A * p2[None, :] + (Bc * Bc)[None, :] * x2[:, None] - 2.0 * A * Bc[None, :] * px) / (den * den), EPS)
    sc_diff_a = (-A * pa[None, :] + Bc[None, :] * xa) / den

    num = 2.0 * sc_diff_a
    denom = clamp_abs((1.0 + k * diff_norm2) * a_norm[None, :])
    distance = arcsinh(sqrt_k * num / denom) / sqrt_k
    return -distance

@@ -1,0 +1,189 @@
+from contextlib import ExitStack
+
+import concourse.bass as bass
+import concourse.mybir as mybir
+import concourse.tile as tile
+from concourse.masks import make_identity
+
+F32 = mybir.dt.float32
+BF16 = mybir.dt.bfloat16
+U32 = mybir.dt.uint32
+U8 = mybir.dt.uint8
+FP8X4 = mybir.dt.float8_e4m3fn_x4
+ALU = mybir.AluOpType
+ACT = mybir.ActivationFunctionType
+AX = mybir.AxisListType
+
+B, D, C = 8192, 512, 128
+P = 128
+NT = B // P
+CT = 4
+NCH = NT // CT
+KB = D // P
+MAXN = 1.0 - 1e-5
+FLOPS = 2 * B * D * 2 * C
+
+EVAC_ON_SCALAR = ((1, 1), (1, 0), (1, 1), (1, 0))
+
+
+def tile_hyperbolicmlr_t_kernel(tc, x, a, p, out):
+    nc = tc.nc
+    xv = x.rearrange("(q g) k -> q g k", g=NT)
+    ov = out.rearrange("(q g) c -> q g c", g=NT)
+    with ExitStack() as ctx:
+        const = ctx.enter_context(tc.tile_pool(name="const", bufs=1))
+        keep = ctx.enter_context(tc.tile_pool(name="keep", bufs=1))
+        xin = ctx.enter_context(tc.tile_pool(name="xin", bufs=4))
+        small = ctx.enter_context(tc.tile_pool(name="small", bufs=4))
+        work = ctx.enter_context(tc.tile_pool(name="work", bufs=3))
+        ps_set = ctx.enter_context(tc.psum_pool(name="ps_set", bufs=1))
+        ps_t = ctx.enter_context(tc.psum_pool(name="ps_t", bufs=3))
+        ps_u = ctx.enter_context(tc.psum_pool(name="ps_u", bufs=2))
+        ps_v = ctx.enter_context(tc.psum_pool(name="ps_v", bufs=2))
+
+        pw = const.tile([P, D], BF16)
+        aw = const.tile([P, D], BF16)
+        nc.sync.dma_start(out=pw[:], in_=p)
+        nc.sync.dma_start(out=aw[:], in_=a)
+
+        one1 = const.tile([P, 1], F32)
+        nc.vector.memset(one1[:], 1.0)
+        warm = const.tile([P, 1], F32)
+        nc.scalar.activation(out=warm[:], in_=one1[:], func=ACT.Sqrt)
+
+        ident_b = const.tile([P, P], BF16)
+        make_identity(nc, ident_b[:])
+        ident_f = const.tile([P, P], F32)
+        make_identity(nc, ident_f[:])
+
+        junk_w = const.tile([P, D], BF16)
+        sums = const.tile([P, 2], F32)
+        nc.scalar.activation(out=junk_w[:], in_=pw[:], func=ACT.Square, accum_out=sums[:, 0:1])
+        nc.scalar.activation(out=junk_w[:], in_=aw[:], func=ACT.Square, accum_out=sums[:, 1:2])
+        prod = const.tile([P, D], F32)
+        nc.vector.tensor_tensor(out=prod[:], in0=pw[:], in1=aw[:], op=ALU.mult)
+        pa = const.tile([P, 1], F32)
+        nc.vector.reduce_sum(out=pa[:], in_=prod[:], axis=AX.X)
+        an = const.tile([P, 1], F32)
+        nc.scalar.activation(out=an[:], in_=sums[:, 1:2], func=ACT.Sqrt)
+        ran = const.tile([P, 1], F32)
+        nc.vector.reciprocal(out=ran[:], in_=an[:])
+        bc = const.tile([P, 1], F32)
+        nc.vector.tensor_scalar(out=bc[:], in0=sums[:, 0:1], scalar1=-1.0, scalar2=1.0, op0=ALU.mult, op1=ALU.add)
+        kc = const.tile([P, 3], F32)
+        nc.vector.tensor_scalar(out=kc[:, 0:1], in0=bc[:], scalar1=ran[:, 0:1], scalar2=-1.0, op0=ALU.mult, op1=ALU.mult)
+        nc.vector.tensor_scalar(out=kc[:, 1:2], in0=pa[:], scalar1=ran[:, 0:1], scalar2=2.0, op0=ALU.mult, op1=ALU.mult)
+        nc.vector.tensor_scalar(out=kc[:, 2:3], in0=bc[:], scalar1=0.5, scalar2=None, op0=ALU.mult)
+        rep = const.tile([P, 3, P], F32)
+        nc.vector.tensor_copy(out=rep[:], in_=kc[:].unsqueeze(2).to_broadcast([P, 3, P]))
+        pc = ps_set.tile([P, 3, P], F32, tag="set")
+        for j in range(3):
+            nc.tensor.transpose(pc[:, j, :], rep[:, j, :], ident_f[:])
+        ctile = const.tile([P, 3, P], F32)
+        nc.vector.tensor_copy(out=ctile[:], in_=pc[:])
+        na2 = ctile[:, 0, :]
+        gam = ctile[:, 1, :]
+        bet = ctile[:, 2, :]
+
+        pwt = ps_set.tile([P, 2 * KB, P], BF16, tag="set")
+        for w, src in enumerate((pw, aw)):
+            for t in range(KB):
+                nc.tensor.transpose(pwt[:, w * KB + t, :], src[:, t * P:(t + 1) * P], ident_b[:])
+        gw = const.tile([P, 2, P, KB], BF16, align_bytes=64)
+        nc.vector.tensor_copy(out=gw[:], in_=pwt[:].rearrange("k (w t) c -> k w c t", w=2))
+        w_codes = const.tile([P, 2 * P], U32, align_bytes=64)
+        w_scales = const.tile([P, 2 * P], U8, align_bytes=64)
+        nc.vector.quantize_mx(out=w_codes[:].bitcast(FP8X4), scales=w_scales[:], in_=gw[:].rearrange("k w c t -> k (w c t)"))
+
+        th_all = []
+        wm_all = []
+        last_hyp = None
+        for c in range(NCH):
+            xr = xin.tile([P, CT, D], BF16)
+            nc.sync.dma_start(out=xr[:], in_=xv[:, c * CT:(c + 1) * CT, :])
+            n2 = small.tile([P, CT], F32)
+            for j in range(CT):
+                junk = work.tile([P, D], BF16, tag="junk")
+                nc.scalar.activation(out=junk[:], in_=xr[:, j, :], func=ACT.Square, accum_out=n2[:, j:j + 1])
+            n2c = small.tile([P, CT], F32)
+            nc.vector.tensor_scalar(out=n2c[:], in0=n2[:], scalar1=1e-30, scalar2=None, op0=ALU.max)
+            nr = small.tile([P, CT], F32)
+            nc.scalar.activation(out=nr[:], in_=n2c[:], func=ACT.Sqrt)
+            rn = small.tile([P, CT], F32)
+            nc.vector.reciprocal(out=rn[:], in_=nr[:])
+            sc = small.tile([P, CT], F32)
+            nc.vector.tensor_scalar(out=sc[:], in0=rn[:], scalar1=MAXN, scalar2=1.0, op0=ALU.mult, op1=ALU.min)
+            x2 = small.tile([P, CT], F32)
+            nc.vector.tensor_scalar(out=x2[:], in0=n2[:], scalar1=MAXN * MAXN, scalar2=None, op0=ALU.min)
+            hb = small.tile([P, CT], F32)
+            nc.vector.tensor_scalar(out=hb[:], in0=x2[:], scalar1=0.5, scalar2=0.5, op0=ALU.mult, op1=ALU.add)
+            omx = small.tile([P, CT], F32)
+            nc.vector.tensor_scalar(out=omx[:], in0=x2[:], scalar1=-1.0, scalar2=1.0, op0=ALU.mult, op1=ALU.add)
+            xs = work.tile([P, CT, D], BF16)
+            for j in range(CT):
+                nc.vector.tensor_scalar(out=xs[:, j, :], in0=xr[:, j, :], scalar1=sc[:, j:j + 1], scalar2=None, op0=ALU.mult)
+            gx = work.tile([P, CT, P, KB], BF16, align_bytes=64)
+            for h in range(CT // 2):
+                pt = ps_t.tile([P, 2 * KB, P], BF16)
+                for jj in range(2):
+                    for t in range(KB):
+                        nc.tensor.transpose(pt[:, jj * KB + t, :], xs[:, 2 * h + jj, t * P:(t + 1) * P], ident_b[:])
+                src = pt[:].rearrange("k (j t) r -> k j r t", j=2)
+                dst = gx[:, 2 * h:2 * h + 2, :, :]
+                if EVAC_ON_SCALAR[c % 4][h]:
+                    nc.scalar.copy(out=dst, in_=src)
+                else:
+                    nc.vector.tensor_copy(out=dst, in_=src)
+            codes = work.tile([P, CT * P], U32, align_bytes=64)
+            scales = work.tile([P, CT * P], U8, align_bytes=64)
+            nc.vector.quantize_mx(out=codes[:].bitcast(FP8X4), scales=scales[:], in_=gx[:].rearrange("k j r t -> k (j r t)"))
+            pu = ps_u.tile([P, CT, P], F32)
+            pv = ps_v.tile([P, CT, P], F32)
+            for j in range(CT):
+                cols = slice(j * P, (j + 1) * P)
+                for w, dstp in enumerate((pu, pv)):
+                    nc.tensor.matmul_mx(
+                        out=dstp[:, j, :],
+                        lhsT=codes[:, cols].bitcast(FP8X4),
+                        lhsT_scale=scales[:, cols],
+                        rhs=w_codes[:, w * P:(w + 1) * P].bitcast(FP8X4),
+                        rhs_scale=w_scales[:, w * P:(w + 1) * P],
+                        start=True,
+                        stop=True,
+                    )
+            ub = work.tile([P, CT, P], F32)
+            nc.scalar.activation(out=ub[:], in_=pu[:], func=ACT.Identity, scale=-1.0)
+            va = work.tile([P, CT, P], F32)
+            nc.vector.tensor_tensor(out=va[:], in0=pv[:], in1=na2.unsqueeze(1).to_broadcast([P, CT, P]), op=ALU.mult)
+            mh = work.tile([P, CT, P], F32)
+            ee = work.tile([P, CT, P], F32)
+            for j in range(CT):
+                nc.vector.scalar_tensor_tensor(out=mh[:, j, :], in0=ub[:, j, :], scalar=hb[:, j:j + 1], in1=gam, op0=ALU.add, op1=ALU.mult)
+                nc.vector.scalar_tensor_tensor(out=ee[:, j, :], in0=ub[:, j, :], scalar=hb[:, j:j + 1], in1=bet, op0=ALU.add, op1=ALU.subtract)
+            nc.vector.tensor_tensor(out=mh[:], in0=mh[:], in1=va[:], op=ALU.add)
+            nc.vector.scalar_tensor_tensor(out=ee[:], in0=ee[:], scalar=0.0, in1=ee[:], op0=ALU.max, op1=ALU.add)
+            th = keep.tile([P, CT, P], F32, name="th%d" % c)
+            for j in range(CT):
+                nc.vector.scalar_tensor_tensor(out=th[:, j, :], in0=bet, scalar=omx[:, j:j + 1], in1=ee[:, j, :], op0=ALU.mult, op1=ALU.add)
+            sn = work.tile([P, CT, P], F32)
+            nc.scalar.activation(out=sn[:], in_=mh[:], func=ACT.Square)
+            st = work.tile([P, CT, P], F32)
+            nc.scalar.activation(out=st[:], in_=th[:], func=ACT.Square)
+            nc.vector.tensor_tensor(out=sn[:], in0=sn[:], in1=st[:], op=ALU.add)
+            hyp = work.tile([P, CT, P], F32)
+            nc.scalar.activation(out=hyp[:], in_=sn[:], func=ACT.Sqrt)
+            wm = keep.tile([P, CT, P], F32, name="wm%d" % c)
+            nc.vector.tensor_tensor(out=wm[:], in0=hyp[:], in1=mh[:], op=ALU.add)
+            th_all.append(th)
+            wm_all.append(wm)
+            last_hyp = hyp
+
+        zb = const.tile([P, 1], F32)
+        nc.vector.tensor_scalar(out=zb[:], in0=last_hyp[:, 0, 0:1], scalar1=0.0, scalar2=0.0, op0=ALU.max, op1=ALU.min)
+        for c in range(NCH):
+            l1 = work.tile([P, CT, P], F32)
+            nc.scalar.activation(out=l1[:], in_=wm_all[c][:], func=ACT.Ln, bias=zb[:, 0:1])
+            l2 = work.tile([P, CT, P], F32)
+            nc.scalar.activation(out=l2[:], in_=th_all[c][:], func=ACT.Ln, bias=zb[:, 0:1])
+            nc.vector.tensor_tensor(out=l1[:], in0=l1[:], in1=l2[:], op=ALU.subtract)
+            nc.sync.dma_start(out=ov[:, c * CT:(c + 1) * CT, :], in_=l1[:])

@@ -1,8 +1,6 @@
 from contextlib import ExitStack
 
-import concourse.bass as bass
 import concourse.mybir as mybir
-import concourse.tile as tile
 from concourse.masks import make_identity
 
 F32 = mybir.dt.float32
@@ -17,173 +15,291 @@ AX = mybir.AxisListType
 B, D, C = 8192, 512, 128
 P = 128
 NT = B // P
-CT = 4
-NCH = NT // CT
 KB = D // P
 MAXN = 1.0 - 1e-5
 FLOPS = 2 * B * D * 2 * C
 
-EVAC_ON_SCALAR = ((1, 1), (1, 0), (1, 1), (1, 0))
+SIZES = (1, 1, 2) + (4,) * 15
+NCH = len(SIZES)
+STARTS = tuple(sum(SIZES[:i]) for i in range(NCH))
+CMAX = max(SIZES)
+PRE = 5
+HY_START = 13
+HY_PER = 3
+LEAD = 2
+
+
+def evac_on_vector(c, h):
+    return c < 5 or (h == 1 and c % 3 == 0)
 
 
 def tile_hyperbolicmlr_t_kernel(tc, x, a, p, out):
     nc = tc.nc
+    assert sum(SIZES) == NT
     xv = x.rearrange("(q g) k -> q g k", g=NT)
     ov = out.rearrange("(q g) c -> q g c", g=NT)
     with ExitStack() as ctx:
         const = ctx.enter_context(tc.tile_pool(name="const", bufs=1))
         keep = ctx.enter_context(tc.tile_pool(name="keep", bufs=1))
-        xin = ctx.enter_context(tc.tile_pool(name="xin", bufs=4))
-        small = ctx.enter_context(tc.tile_pool(name="small", bufs=4))
-        work = ctx.enter_context(tc.tile_pool(name="work", bufs=3))
-        ps_set = ctx.enter_context(tc.psum_pool(name="ps_set", bufs=1))
-        ps_t = ctx.enter_context(tc.psum_pool(name="ps_t", bufs=3))
+        xin = ctx.enter_context(tc.tile_pool(name="xin", bufs=8))
+        small = ctx.enter_context(tc.tile_pool(name="small", bufs=8))
+        work = ctx.enter_context(tc.tile_pool(name="work", bufs=2))
+        work3 = ctx.enter_context(tc.tile_pool(name="work3", bufs=3))
+        ps_t = ctx.enter_context(tc.psum_pool(name="ps_t", bufs=4))
         ps_u = ctx.enter_context(tc.psum_pool(name="ps_u", bufs=2))
         ps_v = ctx.enter_context(tc.psum_pool(name="ps_v", bufs=2))
+        ctx.enter_context(tc.manual_schedule())
 
-        pw = const.tile([P, D], BF16)
-        aw = const.tile([P, D], BF16)
-        nc.sync.dma_start(out=pw[:], in_=p)
-        nc.sync.dma_start(out=aw[:], in_=a)
+        T = {}
 
-        one1 = const.tile([P, 1], F32)
-        nc.vector.memset(one1[:], 1.0)
-        warm = const.tile([P, 1], F32)
-        nc.scalar.activation(out=warm[:], in_=one1[:], func=ACT.Sqrt)
+        def ok(c):
+            return 0 <= c < NCH
 
-        ident_b = const.tile([P, P], BF16)
-        make_identity(nc, ident_b[:])
-        ident_f = const.tile([P, P], F32)
-        make_identity(nc, ident_f[:])
+        def load(c):
+            n = SIZES[c]
+            xr = xin.tile([P, n, D], BF16, name="xr")
+            nc.sync.dma_start(out=xr[:], in_=xv[:, STARTS[c]:STARTS[c] + n, :])
+            T["xr", c] = xr
 
-        junk_w = const.tile([P, D], BF16)
-        sums = const.tile([P, 2], F32)
-        nc.scalar.activation(out=junk_w[:], in_=pw[:], func=ACT.Square, accum_out=sums[:, 0:1])
-        nc.scalar.activation(out=junk_w[:], in_=aw[:], func=ACT.Square, accum_out=sums[:, 1:2])
-        prod = const.tile([P, D], F32)
-        nc.vector.tensor_tensor(out=prod[:], in0=pw[:], in1=aw[:], op=ALU.mult)
-        pa = const.tile([P, 1], F32)
-        nc.vector.reduce_sum(out=pa[:], in_=prod[:], axis=AX.X)
-        an = const.tile([P, 1], F32)
-        nc.scalar.activation(out=an[:], in_=sums[:, 1:2], func=ACT.Sqrt)
-        ran = const.tile([P, 1], F32)
-        nc.vector.reciprocal(out=ran[:], in_=an[:])
-        bc = const.tile([P, 1], F32)
-        nc.vector.tensor_scalar(out=bc[:], in0=sums[:, 0:1], scalar1=-1.0, scalar2=1.0, op0=ALU.mult, op1=ALU.add)
-        kc = const.tile([P, 3], F32)
-        nc.vector.tensor_scalar(out=kc[:, 0:1], in0=bc[:], scalar1=ran[:, 0:1], scalar2=-1.0, op0=ALU.mult, op1=ALU.mult)
-        nc.vector.tensor_scalar(out=kc[:, 1:2], in0=pa[:], scalar1=ran[:, 0:1], scalar2=2.0, op0=ALU.mult, op1=ALU.mult)
-        nc.vector.tensor_scalar(out=kc[:, 2:3], in0=bc[:], scalar1=0.5, scalar2=None, op0=ALU.mult)
-        rep = const.tile([P, 3, P], F32)
-        nc.vector.tensor_copy(out=rep[:], in_=kc[:].unsqueeze(2).to_broadcast([P, 3, P]))
-        pc = ps_set.tile([P, 3, P], F32, tag="set")
-        for j in range(3):
-            nc.tensor.transpose(pc[:, j, :], rep[:, j, :], ident_f[:])
-        ctile = const.tile([P, 3, P], F32)
-        nc.vector.tensor_copy(out=ctile[:], in_=pc[:])
-        na2 = ctile[:, 0, :]
-        gam = ctile[:, 1, :]
-        bet = ctile[:, 2, :]
+        def norms(c):
+            n = SIZES[c]
+            n2 = small.tile([P, n], F32, name="n2")
+            for j in range(n):
+                junk = work.tile([P, D], BF16, name="junk")
+                nc.scalar.activation(out=junk[:], in_=T["xr", c][:, j, :], func=ACT.Square, accum_out=n2[:, j:j + 1])
+            T["n2", c] = n2
 
-        pwt = ps_set.tile([P, 2 * KB, P], BF16, tag="set")
-        for w, src in enumerate((pw, aw)):
-            for t in range(KB):
-                nc.tensor.transpose(pwt[:, w * KB + t, :], src[:, t * P:(t + 1) * P], ident_b[:])
-        gw = const.tile([P, 2, P, KB], BF16, align_bytes=64)
-        nc.vector.tensor_copy(out=gw[:], in_=pwt[:].rearrange("k (w t) c -> k w c t", w=2))
-        w_codes = const.tile([P, 2 * P], U32, align_bytes=64)
-        w_scales = const.tile([P, 2 * P], U8, align_bytes=64)
-        nc.vector.quantize_mx(out=w_codes[:].bitcast(FP8X4), scales=w_scales[:], in_=gw[:].rearrange("k w c t -> k (w c t)"))
+        def floor_n2(c):
+            n = SIZES[c]
+            n2c = small.tile([P, n], F32, name="n2c")
+            nc.vector.tensor_scalar(out=n2c[:], in0=T["n2", c][:], scalar1=1e-30, scalar2=None, op0=ALU.max)
+            T["n2c", c] = n2c
+            x2 = small.tile([P, n], F32, name="x2")
+            nc.gpsimd.tensor_scalar(out=x2[:], in0=T["n2", c][:], scalar1=MAXN * MAXN, scalar2=None, op0=ALU.min)
+            hb = small.tile([P, n], F32, name="hb")
+            nc.gpsimd.tensor_scalar(out=hb[:], in0=x2[:], scalar1=0.5, scalar2=0.5, op0=ALU.mult, op1=ALU.add)
+            omx = small.tile([P, n], F32, name="omx")
+            nc.gpsimd.tensor_scalar(out=omx[:], in0=x2[:], scalar1=-1.0, scalar2=1.0, op0=ALU.mult, op1=ALU.add)
+            T["hb", c] = hb
+            T["omx", c] = omx
 
-        th_all = []
-        wm_all = []
-        last_hyp = None
-        for c in range(NCH):
-            xr = xin.tile([P, CT, D], BF16)
-            nc.sync.dma_start(out=xr[:], in_=xv[:, c * CT:(c + 1) * CT, :])
-            n2 = small.tile([P, CT], F32)
-            for j in range(CT):
-                junk = work.tile([P, D], BF16, tag="junk")
-                nc.scalar.activation(out=junk[:], in_=xr[:, j, :], func=ACT.Square, accum_out=n2[:, j:j + 1])
-            n2c = small.tile([P, CT], F32)
-            nc.vector.tensor_scalar(out=n2c[:], in0=n2[:], scalar1=1e-30, scalar2=None, op0=ALU.max)
-            nr = small.tile([P, CT], F32)
-            nc.scalar.activation(out=nr[:], in_=n2c[:], func=ACT.Sqrt)
-            rn = small.tile([P, CT], F32)
-            nc.vector.reciprocal(out=rn[:], in_=nr[:])
-            sc = small.tile([P, CT], F32)
-            nc.vector.tensor_scalar(out=sc[:], in0=rn[:], scalar1=MAXN, scalar2=1.0, op0=ALU.mult, op1=ALU.min)
-            x2 = small.tile([P, CT], F32)
-            nc.vector.tensor_scalar(out=x2[:], in0=n2[:], scalar1=MAXN * MAXN, scalar2=None, op0=ALU.min)
-            hb = small.tile([P, CT], F32)
-            nc.vector.tensor_scalar(out=hb[:], in0=x2[:], scalar1=0.5, scalar2=0.5, op0=ALU.mult, op1=ALU.add)
-            omx = small.tile([P, CT], F32)
-            nc.vector.tensor_scalar(out=omx[:], in0=x2[:], scalar1=-1.0, scalar2=1.0, op0=ALU.mult, op1=ALU.add)
-            xs = work.tile([P, CT, D], BF16)
-            for j in range(CT):
-                nc.vector.tensor_scalar(out=xs[:, j, :], in0=xr[:, j, :], scalar1=sc[:, j:j + 1], scalar2=None, op0=ALU.mult)
-            gx = work.tile([P, CT, P, KB], BF16, align_bytes=64)
-            for h in range(CT // 2):
-                pt = ps_t.tile([P, 2 * KB, P], BF16)
-                for jj in range(2):
+        def root(c):
+            nr = small.tile([P, SIZES[c]], F32, name="nr")
+            nc.scalar.activation(out=nr[:], in_=T["n2c", c][:], func=ACT.Sqrt)
+            T["nr", c] = nr
+
+        def recip(c):
+            rn = small.tile([P, SIZES[c]], F32, name="rn")
+            nc.vector.reciprocal(out=rn[:], in_=T["nr", c][:])
+            T["rn", c] = rn
+
+        def factor(c):
+            sc = small.tile([P, SIZES[c]], F32, name="sc")
+            nc.vector.tensor_scalar(out=sc[:], in0=T["rn", c][:], scalar1=MAXN, scalar2=1.0, op0=ALU.mult, op1=ALU.min)
+            T["sc", c] = sc
+
+        def scale(c):
+            n = SIZES[c]
+            xs = work.tile([P, n, D], BF16, name="xs")
+            for j in range(n):
+                nc.vector.tensor_scalar(out=xs[:, j, :], in0=T["xr", c][:, j, :], scalar1=T["sc", c][:, j:j + 1], scalar2=None, op0=ALU.mult)
+            T["xs", c] = xs
+
+        def banks(c):
+            n = SIZES[c]
+            return [(h, min(2, n - 2 * h)) for h in range((n + 1) // 2)]
+
+        def transp(c):
+            for h, m in banks(c):
+                pt = ps_t.tile([P, m * KB, P], BF16, name="pt")
+                for jj in range(m):
                     for t in range(KB):
-                        nc.tensor.transpose(pt[:, jj * KB + t, :], xs[:, 2 * h + jj, t * P:(t + 1) * P], ident_b[:])
-                src = pt[:].rearrange("k (j t) r -> k j r t", j=2)
-                dst = gx[:, 2 * h:2 * h + 2, :, :]
-                if EVAC_ON_SCALAR[c % 4][h]:
-                    nc.scalar.copy(out=dst, in_=src)
-                else:
+                        nc.tensor.transpose(pt[:, jj * KB + t, :], T["xs", c][:, 2 * h + jj, t * P:(t + 1) * P], ident_b[:])
+                T["pt", c, h] = pt
+
+        def evac(c, on_vector):
+            if ("gx", c) not in T:
+                T["gx", c] = work3.tile([P, SIZES[c], P, KB], BF16, name="gx", align_bytes=64)
+            for h, m in banks(c):
+                if evac_on_vector(c, h) != on_vector:
+                    continue
+                src = T["pt", c, h][:].rearrange("k (j t) r -> k j r t", j=m)
+                dst = T["gx", c][:, 2 * h:2 * h + m, :, :]
+                if on_vector:
                     nc.vector.tensor_copy(out=dst, in_=src)
-            codes = work.tile([P, CT * P], U32, align_bytes=64)
-            scales = work.tile([P, CT * P], U8, align_bytes=64)
-            nc.vector.quantize_mx(out=codes[:].bitcast(FP8X4), scales=scales[:], in_=gx[:].rearrange("k j r t -> k (j r t)"))
-            pu = ps_u.tile([P, CT, P], F32)
-            pv = ps_v.tile([P, CT, P], F32)
-            for j in range(CT):
+                else:
+                    nc.scalar.copy(out=dst, in_=src)
+
+        def quant(c):
+            n = SIZES[c]
+            codes = work.tile([P, n * P], U32, name="codes", align_bytes=64)
+            scales = work.tile([P, n * P], U8, name="scales", align_bytes=64)
+            nc.vector.quantize_mx(out=codes[:].bitcast(FP8X4), scales=scales[:], in_=T["gx", c][:].rearrange("k j r t -> k (j r t)"))
+            T["codes", c] = codes
+            T["scales", c] = scales
+
+        def mx(c):
+            n = SIZES[c]
+            pu = ps_u.tile([P, n, P], F32, name="pu")
+            pv = ps_v.tile([P, n, P], F32, name="pv")
+            for j in range(n):
                 cols = slice(j * P, (j + 1) * P)
                 for w, dstp in enumerate((pu, pv)):
                     nc.tensor.matmul_mx(
                         out=dstp[:, j, :],
-                        lhsT=codes[:, cols].bitcast(FP8X4),
-                        lhsT_scale=scales[:, cols],
+                        lhsT=T["codes", c][:, cols].bitcast(FP8X4),
+                        lhsT_scale=T["scales", c][:, cols],
                         rhs=w_codes[:, w * P:(w + 1) * P].bitcast(FP8X4),
                         rhs_scale=w_scales[:, w * P:(w + 1) * P],
                         start=True,
                         stop=True,
                     )
-            ub = work.tile([P, CT, P], F32)
-            nc.scalar.activation(out=ub[:], in_=pu[:], func=ACT.Identity, scale=-1.0)
-            va = work.tile([P, CT, P], F32)
-            nc.vector.tensor_tensor(out=va[:], in0=pv[:], in1=na2.unsqueeze(1).to_broadcast([P, CT, P]), op=ALU.mult)
-            mh = work.tile([P, CT, P], F32)
-            ee = work.tile([P, CT, P], F32)
-            for j in range(CT):
-                nc.vector.scalar_tensor_tensor(out=mh[:, j, :], in0=ub[:, j, :], scalar=hb[:, j:j + 1], in1=gam, op0=ALU.add, op1=ALU.mult)
-                nc.vector.scalar_tensor_tensor(out=ee[:, j, :], in0=ub[:, j, :], scalar=hb[:, j:j + 1], in1=bet, op0=ALU.add, op1=ALU.subtract)
-            nc.vector.tensor_tensor(out=mh[:], in0=mh[:], in1=va[:], op=ALU.add)
-            nc.vector.scalar_tensor_tensor(out=ee[:], in0=ee[:], scalar=0.0, in1=ee[:], op0=ALU.max, op1=ALU.add)
-            th = keep.tile([P, CT, P], F32, name="th%d" % c)
-            for j in range(CT):
-                nc.vector.scalar_tensor_tensor(out=th[:, j, :], in0=bet, scalar=omx[:, j:j + 1], in1=ee[:, j, :], op0=ALU.mult, op1=ALU.add)
-            sn = work.tile([P, CT, P], F32)
-            nc.scalar.activation(out=sn[:], in_=mh[:], func=ACT.Square)
-            st = work.tile([P, CT, P], F32)
-            nc.scalar.activation(out=st[:], in_=th[:], func=ACT.Square)
-            nc.vector.tensor_tensor(out=sn[:], in0=sn[:], in1=st[:], op=ALU.add)
-            hyp = work.tile([P, CT, P], F32)
-            nc.scalar.activation(out=hyp[:], in_=sn[:], func=ACT.Sqrt)
-            wm = keep.tile([P, CT, P], F32, name="wm%d" % c)
-            nc.vector.tensor_tensor(out=wm[:], in0=hyp[:], in1=mh[:], op=ALU.add)
-            th_all.append(th)
-            wm_all.append(wm)
-            last_hyp = hyp
+            T["pu", c] = pu
+            T["pv", c] = pv
 
-        zb = const.tile([P, 1], F32)
-        nc.vector.tensor_scalar(out=zb[:], in0=last_hyp[:, 0, 0:1], scalar1=0.0, scalar2=0.0, op0=ALU.max, op1=ALU.min)
-        for c in range(NCH):
-            l1 = work.tile([P, CT, P], F32)
-            nc.scalar.activation(out=l1[:], in_=wm_all[c][:], func=ACT.Ln, bias=zb[:, 0:1])
-            l2 = work.tile([P, CT, P], F32)
-            nc.scalar.activation(out=l2[:], in_=th_all[c][:], func=ACT.Ln, bias=zb[:, 0:1])
-            nc.vector.tensor_tensor(out=l1[:], in0=l1[:], in1=l2[:], op=ALU.subtract)
-            nc.sync.dma_start(out=ov[:, c * CT:(c + 1) * CT, :], in_=l1[:])
+        def step3(c):
+            n = SIZES[c]
+            mh = keep.tile([P, n, P], F32, name="mh%d" % c)
+            ee = work.tile([P, n, P], F32, name="ee")
+            va = work.tile([P, n, P], F32, name="va")
+            th = keep.tile([P, n, P], F32, name="th%d" % c)
+            hb = T["hb", c]
+            for j in reversed(range(n)):
+                nc.vector.scalar_tensor_tensor(out=mh[:, j, :], in0=T["pu", c][:, j, :], scalar=hb[:, j:j + 1], in1=ngam, op0=ALU.subtract, op1=ALU.mult)
+            for j in range(n):
+                nc.vector.scalar_tensor_tensor(out=ee[:, j, :], in0=nbet, scalar=hb[:, j:j + 1], in1=T["pu", c][:, j, :], op0=ALU.add, op1=ALU.subtract)
+            nc.vector.tensor_tensor(out=va[:], in0=T["pv", c][:], in1=na2.unsqueeze(1).to_broadcast([P, n, P]), op=ALU.mult)
+            nc.vector.scalar_tensor_tensor(out=ee[:], in0=ee[:], scalar=0.0, in1=ee[:], op0=ALU.max, op1=ALU.add)
+            nc.vector.tensor_tensor(out=mh[:], in0=mh[:], in1=va[:], op=ALU.add)
+            for j in range(n):
+                nc.vector.scalar_tensor_tensor(out=th[:, j, :], in0=bet, scalar=T["omx", c][:, j:j + 1], in1=ee[:, j, :], op0=ALU.mult, op1=ALU.add)
+            T["mh", c] = mh
+            T["th", c] = th
+
+        def squares(c):
+            n = SIZES[c]
+            sn = keep.tile([P, n, P], F32, name="sn%d" % c)
+            nc.scalar.activation(out=sn[:], in_=T["mh", c][:], func=ACT.Square)
+            st = work3.tile([P, n, P], F32, name="st")
+            nc.scalar.activation(out=st[:], in_=T["th", c][:], func=ACT.Square)
+            T["sn", c] = sn
+            T["st", c] = st
+
+        def sumsq(c):
+            nc.vector.tensor_tensor(out=T["sn", c][:], in0=T["sn", c][:], in1=T["st", c][:], op=ALU.add)
+
+        def hypot(c):
+            nc.scalar.activation(out=T["sn", c][:], in_=T["sn", c][:], func=ACT.Sqrt)
+
+        load(0)
+        pw = const.tile([P, D], BF16)
+        aw = const.tile([P, D], BF16)
+        nc.sync.dma_start(out=pw[:], in_=p)
+        nc.sync.dma_start(out=aw[:], in_=a)
+        for c in range(1, PRE):
+            load(c)
+        one1 = const.tile([P, 1], F32)
+        nc.vector.memset(one1[:], 1.0)
+        warm = const.tile([P, 1], F32)
+        nc.scalar.activation(out=warm[:], in_=one1[:], func=ACT.Sqrt)
+        ident_b = const.tile([P, P], BF16)
+        make_identity(nc, ident_b[:])
+        ident_f = const.tile([P, P], F32)
+        make_identity(nc, ident_f[:])
+
+        sums = const.tile([P, 2], F32)
+        an = const.tile([P, 1], F32)
+        ctile = const.tile([P, 4, P], F32)
+        na2 = ctile[:, 0, :]
+        ngam = ctile[:, 1, :]
+        bet = ctile[:, 2, :]
+        nbet = ctile[:, 3, :]
+        w_codes = const.tile([P, 2 * P], U32, align_bytes=64)
+        w_scales = const.tile([P, 2 * P], U8, align_bytes=64)
+
+        def setup_scalar():
+            junk_w = const.tile([P, D], BF16)
+            nc.scalar.activation(out=junk_w[:], in_=pw[:], func=ACT.Square, accum_out=sums[:, 0:1])
+            nc.scalar.activation(out=junk_w[:], in_=aw[:], func=ACT.Square, accum_out=sums[:, 1:2])
+            nc.scalar.activation(out=an[:], in_=sums[:, 1:2], func=ACT.Sqrt)
+
+        def setup_rest():
+            pwt = ps_t.tile([P, 2 * KB, P], BF16, name="pt")
+            for w, src in enumerate((pw, aw)):
+                for t in range(KB):
+                    nc.tensor.transpose(pwt[:, w * KB + t, :], src[:, t * P:(t + 1) * P], ident_b[:])
+            gw = const.tile([P, 2, P, KB], BF16, align_bytes=64)
+            nc.vector.tensor_copy(out=gw[:], in_=pwt[:].rearrange("k (w t) c -> k w c t", w=2))
+            prod = const.tile([P, D], F32)
+            nc.vector.tensor_tensor(out=prod[:], in0=pw[:], in1=aw[:], op=ALU.mult)
+            nc.vector.quantize_mx(out=w_codes[:].bitcast(FP8X4), scales=w_scales[:], in_=gw[:].rearrange("k w c t -> k (w c t)"))
+            pa = const.tile([P, 1], F32)
+            nc.vector.reduce_sum(out=pa[:], in_=prod[:], axis=AX.X)
+            ran = const.tile([P, 1], F32)
+            nc.vector.reciprocal(out=ran[:], in_=an[:])
+            bc = const.tile([P, 1], F32)
+            nc.vector.tensor_scalar(out=bc[:], in0=sums[:, 0:1], scalar1=-1.0, scalar2=1.0, op0=ALU.mult, op1=ALU.add)
+            kc = const.tile([P, 4], F32)
+            nc.vector.tensor_scalar(out=kc[:, 0:1], in0=bc[:], scalar1=ran[:, 0:1], scalar2=-1.0, op0=ALU.mult, op1=ALU.mult)
+            nc.vector.tensor_scalar(out=kc[:, 1:2], in0=pa[:], scalar1=ran[:, 0:1], scalar2=-2.0, op0=ALU.mult, op1=ALU.mult)
+            nc.vector.tensor_scalar(out=kc[:, 2:3], in0=bc[:], scalar1=0.5, scalar2=None, op0=ALU.mult)
+            nc.vector.tensor_scalar(out=kc[:, 3:4], in0=bc[:], scalar1=-0.5, scalar2=None, op0=ALU.mult)
+            rep = const.tile([P, 4, P], F32)
+            nc.vector.tensor_copy(out=rep[:], in_=kc[:].unsqueeze(2).to_broadcast([P, 4, P]))
+            pc = ps_t.tile([P, 4, P], F32, name="pt")
+            for j in range(4):
+                nc.tensor.transpose(pc[:, j, :], rep[:, j, :], ident_f[:])
+            nc.vector.tensor_copy(out=ctile[:], in_=pc[:])
+
+        nh = 0
+        for k in range(-5, NCH + 3):
+            if ok(k + 5 + PRE):
+                load(k + 5 + PRE)
+            if ok(k + 3):
+                recip(k + 3)
+            if ok(k + 1):
+                quant(k + 1)
+                mx(k + 1)
+            if ok(k + 3):
+                factor(k + 3)
+            if ok(k - 2):
+                sumsq(k - 2)
+            if ok(k + 3):
+                scale(k + 3)
+                transp(k + 3)
+            if k == -3:
+                setup_rest()
+            if ok(k + 2):
+                evac(k + 2, False)
+            if ok(k + 5):
+                norms(k + 5)
+            if ok(k):
+                step3(k)
+            if ok(k - 1):
+                squares(k - 1)
+            if ok(k + 2):
+                evac(k + 2, True)
+            if ok(k + 5):
+                floor_n2(k + 5)
+            if ok(k + 4):
+                root(k + 4)
+            if k == -5:
+                setup_scalar()
+            if k >= HY_START:
+                for i in range(HY_PER):
+                    if nh < NCH and nh <= k - 3:
+                        hypot(nh)
+                        nh += 1
+        while nh < NCH:
+            hypot(nh)
+            nh += 1
+
+        for c in range(NCH + LEAD):
+            if ok(c):
+                nc.vector.tensor_tensor(out=T["sn", c][:], in0=T["sn", c][:], in1=T["mh", c][:], op=ALU.add)
+                nc.scalar.activation(out=T["th", c][:], in_=T["th", c][:], func=ACT.Ln)
+                nc.scalar.activation(out=T["sn", c][:], in_=T["sn", c][:], func=ACT.Ln)
+            d = c - LEAD
+            if ok(d):
+                nc.vector.tensor_tensor(out=T["sn", d][:], in0=T["sn", d][:], in1=T["th", d][:], op=ALU.subtract)
+                nc.sync.dma_start(out=ov[:, STARTS[d]:STARTS[d] + SIZES[d], :], in_=T["sn", d][:])

@@ -19,25 +19,29 @@ KB = D // P
 MAXN = 1.0 - 1e-5
 FLOPS = 2 * B * D * 2 * C
 
-SIZES = (1, 1, 2) + (4,) * 15
+SIZES = (2, 2) + (4,) * 15
 NCH = len(SIZES)
 STARTS = tuple(sum(SIZES[:i]) for i in range(NCH))
 CMAX = max(SIZES)
-PRE = 5
-HY_START = 13
+PRE = 4
+HY_START = 12
 HY_PER = 3
 LEAD = 2
 
 
+HD = D // 2
+HP = P // 2
+
+
 def evac_on_vector(c, h):
-    return c < 5 or (h == 1 and c % 3 == 0)
+    return c < 3
 
 
 def tile_hyperbolicmlr_t_kernel(tc, x, a, p, out):
     nc = tc.nc
     assert sum(SIZES) == NT
-    xv = x.rearrange("(q g) k -> q g k", g=NT)
-    ov = out.rearrange("(q g) c -> q g c", g=NT)
+    xv = x.rearrange("b (u m) -> (b u) m", u=2).rearrange("(G i) m -> i G m", i=P)
+    ov = out.rearrange("(g q) c -> q g c", q=P)
     with ExitStack() as ctx:
         const = ctx.enter_context(tc.tile_pool(name="const", bufs=1))
         keep = ctx.enter_context(tc.tile_pool(name="keep", bufs=1))
@@ -46,8 +50,9 @@ def tile_hyperbolicmlr_t_kernel(tc, x, a, p, out):
         work = ctx.enter_context(tc.tile_pool(name="work", bufs=2))
         work3 = ctx.enter_context(tc.tile_pool(name="work3", bufs=3))
         ps_t = ctx.enter_context(tc.psum_pool(name="ps_t", bufs=4))
-        ps_u = ctx.enter_context(tc.psum_pool(name="ps_u", bufs=2))
-        ps_v = ctx.enter_context(tc.psum_pool(name="ps_v", bufs=2))
+        ps_u = ctx.enter_context(tc.psum_pool(name="ps_u", bufs=1))
+        ps_v = ctx.enter_context(tc.psum_pool(name="ps_v", bufs=1))
+        ps_n = ctx.enter_context(tc.psum_pool(name="ps_n", bufs=2))
         ctx.enter_context(tc.manual_schedule())
 
         T = {}
@@ -57,25 +62,36 @@ def tile_hyperbolicmlr_t_kernel(tc, x, a, p, out):
 
         def load(c):
             n = SIZES[c]
-            xr = xin.tile([P, n, D], BF16, name="xr")
-            nc.sync.dma_start(out=xr[:], in_=xv[:, STARTS[c]:STARTS[c] + n, :])
+            xr = xin.tile([P, 2 * n, HD], BF16, name="xr")
+            nc.sync.dma_start(out=xr[:], in_=xv[:, 2 * STARTS[c]:2 * (STARTS[c] + n), :])
             T["xr", c] = xr
 
         def norms(c):
             n = SIZES[c]
-            n2 = small.tile([P, n], F32, name="n2")
-            for j in range(n):
-                junk = work.tile([P, D], BF16, name="junk")
-                nc.scalar.activation(out=junk[:], in_=T["xr", c][:, j, :], func=ACT.Square, accum_out=n2[:, j:j + 1])
-            T["n2", c] = n2
+            ss = small.tile([P, 2 * n], F32, name="ss")
+            for g in range(2 * n):
+                junk = work.tile([P, HD], BF16, name="junk")
+                nc.scalar.activation(out=junk[:], in_=T["xr", c][:, g, :], func=ACT.Square, accum_out=ss[:, g:g + 1])
+            T["ss", c] = ss
+
+        def rowsums(c):
+            n = SIZES[c]
+            pn = ps_n.tile([P, 3 * n], F32, name="pn")
+            ss = T["ss", c]
+            nc.tensor.matmul(out=pn[:, 0:2 * n], lhsT=pair[:].rearrange("i r u -> i (r u)"), rhs=ss[:], start=True, stop=True)
+            halves = ss[:].rearrange("i (j l) -> i j l", l=2)
+            for l in range(2):
+                nc.tensor.matmul(out=pn[:, 2 * n:3 * n], lhsT=sel[:, l, :], rhs=halves[:, :, l], start=(l == 0), stop=(l == 1))
+            T["pn", c] = pn
 
         def floor_n2(c):
             n = SIZES[c]
-            n2c = small.tile([P, n], F32, name="n2c")
-            nc.vector.tensor_scalar(out=n2c[:], in0=T["n2", c][:], scalar1=1e-30, scalar2=None, op0=ALU.max)
-            T["n2c", c] = n2c
+            pn = T["pn", c]
             x2 = small.tile([P, n], F32, name="x2")
-            nc.gpsimd.tensor_scalar(out=x2[:], in0=T["n2", c][:], scalar1=MAXN * MAXN, scalar2=None, op0=ALU.min)
+            nc.vector.tensor_scalar(out=x2[:], in0=pn[:, 2 * n:3 * n], scalar1=MAXN * MAXN, scalar2=None, op0=ALU.min)
+            n2c = small.tile([P, 2 * n], F32, name="n2c")
+            nc.vector.tensor_scalar(out=n2c[:], in0=pn[:, 0:2 * n], scalar1=1e-30, scalar2=None, op0=ALU.max)
+            T["n2c", c] = n2c
             hb = small.tile([P, n], F32, name="hb")
             nc.gpsimd.tensor_scalar(out=hb[:], in0=x2[:], scalar1=0.5, scalar2=0.5, op0=ALU.mult, op1=ALU.add)
             omx = small.tile([P, n], F32, name="omx")
@@ -84,25 +100,25 @@ def tile_hyperbolicmlr_t_kernel(tc, x, a, p, out):
             T["omx", c] = omx
 
         def root(c):
-            nr = small.tile([P, SIZES[c]], F32, name="nr")
+            nr = small.tile([P, 2 * SIZES[c]], F32, name="nr")
             nc.scalar.activation(out=nr[:], in_=T["n2c", c][:], func=ACT.Sqrt)
             T["nr", c] = nr
 
         def recip(c):
-            rn = small.tile([P, SIZES[c]], F32, name="rn")
+            rn = small.tile([P, 2 * SIZES[c]], F32, name="rn")
             nc.vector.reciprocal(out=rn[:], in_=T["nr", c][:])
             T["rn", c] = rn
 
         def factor(c):
-            sc = small.tile([P, SIZES[c]], F32, name="sc")
+            sc = small.tile([P, 2 * SIZES[c]], F32, name="sc")
             nc.vector.tensor_scalar(out=sc[:], in0=T["rn", c][:], scalar1=MAXN, scalar2=1.0, op0=ALU.mult, op1=ALU.min)
             T["sc", c] = sc
 
         def scale(c):
             n = SIZES[c]
-            xs = work.tile([P, n, D], BF16, name="xs")
-            for j in range(n):
-                nc.vector.tensor_scalar(out=xs[:, j, :], in0=T["xr", c][:, j, :], scalar1=T["sc", c][:, j:j + 1], scalar2=None, op0=ALU.mult)
+            xs = work.tile([P, 2 * n, HD], BF16, name="xs")
+            for g in range(2 * n):
+                nc.vector.tensor_scalar(out=xs[:, g, :], in0=T["xr", c][:, g, :], scalar1=T["sc", c][:, g:g + 1], scalar2=None, op0=ALU.mult)
             T["xs", c] = xs
 
         def banks(c):
@@ -111,20 +127,20 @@ def tile_hyperbolicmlr_t_kernel(tc, x, a, p, out):
 
         def transp(c):
             for h, m in banks(c):
-                pt = ps_t.tile([P, m * KB, P], BF16, name="pt")
-                for jj in range(m):
-                    for t in range(KB):
-                        nc.tensor.transpose(pt[:, jj * KB + t, :], T["xs", c][:, 2 * h + jj, t * P:(t + 1) * P], ident_b[:])
+                pt = ps_t.tile([P, 2, 2 * m, P], BF16, name="pt")
+                for s in range(2 * m):
+                    for v in range(2):
+                        nc.tensor.transpose(pt[:, v, s, :], T["xs", c][:, 4 * h + s, v * P:(v + 1) * P], ident_b[:])
                 T["pt", c, h] = pt
 
         def evac(c, on_vector):
             if ("gx", c) not in T:
-                T["gx", c] = work3.tile([P, SIZES[c], P, KB], BF16, name="gx", align_bytes=64)
+                T["gx", c] = work3.tile([P, SIZES[c] * P, KB], BF16, name="gx", align_bytes=64)
             for h, m in banks(c):
                 if evac_on_vector(c, h) != on_vector:
                     continue
-                src = T["pt", c, h][:].rearrange("k (j t) r -> k j r t", j=m)
-                dst = T["gx", c][:, 2 * h:2 * h + m, :, :]
+                src = T["pt", c, h][:].rearrange("k v s (r u) -> k (s r) v u", u=2)
+                dst = T["gx", c][:, 2 * h * P:(2 * h + m) * P, :].rearrange("k c (v u) -> k c v u", u=2)
                 if on_vector:
                     nc.vector.tensor_copy(out=dst, in_=src)
                 else:
@@ -134,7 +150,7 @@ def tile_hyperbolicmlr_t_kernel(tc, x, a, p, out):
             n = SIZES[c]
             codes = work.tile([P, n * P], U32, name="codes", align_bytes=64)
             scales = work.tile([P, n * P], U8, name="scales", align_bytes=64)
-            nc.vector.quantize_mx(out=codes[:].bitcast(FP8X4), scales=scales[:], in_=T["gx", c][:].rearrange("k j r t -> k (j r t)"))
+            nc.vector.quantize_mx(out=codes[:].bitcast(FP8X4), scales=scales[:], in_=T["gx", c][:].rearrange("k c t -> k (c t)"))
             T["codes", c] = codes
             T["scales", c] = scales
 
@@ -207,6 +223,15 @@ def tile_hyperbolicmlr_t_kernel(tc, x, a, p, out):
         ident_f = const.tile([P, P], F32)
         make_identity(nc, ident_f[:])
 
+        rsel = const.tile([P, HP], F32)
+        nc.vector.reduce_sum(out=rsel[:], in_=ident_f[:].rearrange("i (r u) -> i r u", u=2), axis=AX.X)
+        pair = const.tile([P, HP, 2], F32)
+        nc.vector.tensor_copy(out=pair[:], in_=rsel[:].unsqueeze(2).to_broadcast([P, HP, 2]))
+        sel = const.tile([P, 2, P], F32)
+        nc.vector.memset(sel[:], 0.0)
+        for l in range(2):
+            nc.vector.tensor_copy(out=sel[:, l, l * HP:(l + 1) * HP], in_=rsel[:])
+
         sums = const.tile([P, 2], F32)
         an = const.tile([P, 1], F32)
         ctile = const.tile([P, 4, P], F32)
@@ -229,7 +254,8 @@ def tile_hyperbolicmlr_t_kernel(tc, x, a, p, out):
                 for t in range(KB):
                     nc.tensor.transpose(pwt[:, w * KB + t, :], src[:, t * P:(t + 1) * P], ident_b[:])
             gw = const.tile([P, 2, P, KB], BF16, align_bytes=64)
-            nc.vector.tensor_copy(out=gw[:], in_=pwt[:].rearrange("k (w t) c -> k w c t", w=2))
+            for w in range(2):
+                nc.vector.tensor_copy(out=gw[:, w, :, :].rearrange("k c (v u) -> k c v u", u=2), in_=pwt[:, w * KB:(w + 1) * KB, :].rearrange("k (u v) c -> k c v u", u=2))
             prod = const.tile([P, D], F32)
             nc.vector.tensor_tensor(out=prod[:], in0=pw[:], in1=aw[:], op=ALU.mult)
             nc.vector.quantize_mx(out=w_codes[:].bitcast(FP8X4), scales=w_scales[:], in_=gw[:].rearrange("k w c t -> k (w c t)"))
@@ -252,14 +278,13 @@ def tile_hyperbolicmlr_t_kernel(tc, x, a, p, out):
             nc.vector.tensor_copy(out=ctile[:], in_=pc[:])
 
         nh = 0
-        for k in range(-5, NCH + 3):
-            if ok(k + 5 + PRE):
-                load(k + 5 + PRE)
+        for k in range(-6, NCH + 3):
+            if ok(k + 6 + PRE):
+                load(k + 6 + PRE)
             if ok(k + 3):
                 recip(k + 3)
             if ok(k + 1):
                 quant(k + 1)
-                mx(k + 1)
             if ok(k + 3):
                 factor(k + 3)
             if ok(k - 2):
@@ -269,21 +294,24 @@ def tile_hyperbolicmlr_t_kernel(tc, x, a, p, out):
                 transp(k + 3)
             if k == -3:
                 setup_rest()
+            if ok(k + 4):
+                root(k + 4)
             if ok(k + 2):
                 evac(k + 2, False)
+            if ok(k + 6):
+                norms(k + 6)
+                rowsums(k + 6)
             if ok(k + 5):
-                norms(k + 5)
+                floor_n2(k + 5)
             if ok(k):
                 step3(k)
+            if ok(k + 1):
+                mx(k + 1)
             if ok(k - 1):
                 squares(k - 1)
             if ok(k + 2):
                 evac(k + 2, True)
-            if ok(k + 5):
-                floor_n2(k + 5)
-            if ok(k + 4):
-                root(k + 4)
-            if k == -5:
+            if k == -6:
                 setup_scalar()
             if k >= HY_START:
                 for i in range(HY_PER):

@@ -19,29 +19,25 @@ KB = D // P
 MAXN = 1.0 - 1e-5
 FLOPS = 2 * B * D * 2 * C
 
-SIZES = (2, 2) + (4,) * 15
+SIZES = (1, 1, 2) + (4,) * 15
 NCH = len(SIZES)
 STARTS = tuple(sum(SIZES[:i]) for i in range(NCH))
 CMAX = max(SIZES)
-PRE = 4
-HY_START = 12
+PRE = 5
+HY_START = 13
 HY_PER = 3
 LEAD = 2
 
 
-HD = D // 2
-HP = P // 2
-
-
 def evac_on_vector(c, h):
-    return c < 3
+    return c < 5 or (h == 1 and c % 2 == 0)
 
 
 def tile_hyperbolicmlr_t_kernel(tc, x, a, p, out):
     nc = tc.nc
     assert sum(SIZES) == NT
-    xv = x.rearrange("b (u m) -> (b u) m", u=2).rearrange("(G i) m -> i G m", i=P)
-    ov = out.rearrange("(g q) c -> q g c", q=P)
+    xv = x.rearrange("(q g) k -> q g k", g=NT)
+    ov = out.rearrange("(q g) c -> q g c", g=NT)
     with ExitStack() as ctx:
         const = ctx.enter_context(tc.tile_pool(name="const", bufs=1))
         keep = ctx.enter_context(tc.tile_pool(name="keep", bufs=1))
@@ -50,9 +46,8 @@ def tile_hyperbolicmlr_t_kernel(tc, x, a, p, out):
         work = ctx.enter_context(tc.tile_pool(name="work", bufs=2))
         work3 = ctx.enter_context(tc.tile_pool(name="work3", bufs=3))
         ps_t = ctx.enter_context(tc.psum_pool(name="ps_t", bufs=4))
-        ps_u = ctx.enter_context(tc.psum_pool(name="ps_u", bufs=1))
-        ps_v = ctx.enter_context(tc.psum_pool(name="ps_v", bufs=1))
-        ps_n = ctx.enter_context(tc.psum_pool(name="ps_n", bufs=2))
+        ps_u = ctx.enter_context(tc.psum_pool(name="ps_u", bufs=2))
+        ps_v = ctx.enter_context(tc.psum_pool(name="ps_v", bufs=2))
         ctx.enter_context(tc.manual_schedule())
 
         T = {}
@@ -62,36 +57,25 @@ def tile_hyperbolicmlr_t_kernel(tc, x, a, p, out):
 
         def load(c):
             n = SIZES[c]
-            xr = xin.tile([P, 2 * n, HD], BF16, name="xr")
-            nc.sync.dma_start(out=xr[:], in_=xv[:, 2 * STARTS[c]:2 * (STARTS[c] + n), :])
+            xr = xin.tile([P, n, D], BF16, name="xr")
+            nc.sync.dma_start(out=xr[:], in_=xv[:, STARTS[c]:STARTS[c] + n, :])
             T["xr", c] = xr
 
         def norms(c):
             n = SIZES[c]
-            ss = small.tile([P, 2 * n], F32, name="ss")
-            for g in range(2 * n):
-                junk = work.tile([P, HD], BF16, name="junk")
-                nc.scalar.activation(out=junk[:], in_=T["xr", c][:, g, :], func=ACT.Square, accum_out=ss[:, g:g + 1])
-            T["ss", c] = ss
-
-        def rowsums(c):
-            n = SIZES[c]
-            pn = ps_n.tile([P, 3 * n], F32, name="pn")
-            ss = T["ss", c]
-            nc.tensor.matmul(out=pn[:, 0:2 * n], lhsT=pair[:].rearrange("i r u -> i (r u)"), rhs=ss[:], start=True, stop=True)
-            halves = ss[:].rearrange("i (j l) -> i j l", l=2)
-            for l in range(2):
-                nc.tensor.matmul(out=pn[:, 2 * n:3 * n], lhsT=sel[:, l, :], rhs=halves[:, :, l], start=(l == 0), stop=(l == 1))
-            T["pn", c] = pn
+            n2 = small.tile([P, n], F32, name="n2")
+            for j in range(n):
+                junk = work.tile([P, D], BF16, name="junk")
+                nc.scalar.activation(out=junk[:], in_=T["xr", c][:, j, :], func=ACT.Square, accum_out=n2[:, j:j + 1])
+            T["n2", c] = n2
 
         def floor_n2(c):
             n = SIZES[c]
-            pn = T["pn", c]
-            x2 = small.tile([P, n], F32, name="x2")
-            nc.vector.tensor_scalar(out=x2[:], in0=pn[:, 2 * n:3 * n], scalar1=MAXN * MAXN, scalar2=None, op0=ALU.min)
-            n2c = small.tile([P, 2 * n], F32, name="n2c")
-            nc.vector.tensor_scalar(out=n2c[:], in0=pn[:, 0:2 * n], scalar1=1e-30, scalar2=None, op0=ALU.max)
+            n2c = small.tile([P, n], F32, name="n2c")
+            nc.vector.tensor_scalar(out=n2c[:], in0=T["n2", c][:], scalar1=1e-30, scalar2=None, op0=ALU.max)
             T["n2c", c] = n2c
+            x2 = small.tile([P, n], F32, name="x2")
+            nc.gpsimd.tensor_scalar(out=x2[:], in0=T["n2", c][:], scalar1=MAXN * MAXN, scalar2=None, op0=ALU.min)
             hb = small.tile([P, n], F32, name="hb")
             nc.gpsimd.tensor_scalar(out=hb[:], in0=x2[:], scalar1=0.5, scalar2=0.5, op0=ALU.mult, op1=ALU.add)
             omx = small.tile([P, n], F32, name="omx")
@@ -100,25 +84,25 @@ def tile_hyperbolicmlr_t_kernel(tc, x, a, p, out):
             T["omx", c] = omx
 
         def root(c):
-            nr = small.tile([P, 2 * SIZES[c]], F32, name="nr")
+            nr = small.tile([P, SIZES[c]], F32, name="nr")
             nc.scalar.activation(out=nr[:], in_=T["n2c", c][:], func=ACT.Sqrt)
             T["nr", c] = nr
 
         def recip(c):
-            rn = small.tile([P, 2 * SIZES[c]], F32, name="rn")
+            rn = small.tile([P, SIZES[c]], F32, name="rn")
             nc.vector.reciprocal(out=rn[:], in_=T["nr", c][:])
             T["rn", c] = rn
 
         def factor(c):
-            sc = small.tile([P, 2 * SIZES[c]], F32, name="sc")
+            sc = small.tile([P, SIZES[c]], F32, name="sc")
             nc.vector.tensor_scalar(out=sc[:], in0=T["rn", c][:], scalar1=MAXN, scalar2=1.0, op0=ALU.mult, op1=ALU.min)
             T["sc", c] = sc
 
         def scale(c):
             n = SIZES[c]
-            xs = work.tile([P, 2 * n, HD], BF16, name="xs")
-            for g in range(2 * n):
-                nc.vector.tensor_scalar(out=xs[:, g, :], in0=T["xr", c][:, g, :], scalar1=T["sc", c][:, g:g + 1], scalar2=None, op0=ALU.mult)
+            xs = work.tile([P, n, D], BF16, name="xs")
+            for j in range(n):
+                nc.vector.tensor_scalar(out=xs[:, j, :], in0=T["xr", c][:, j, :], scalar1=T["sc", c][:, j:j + 1], scalar2=None, op0=ALU.mult)
             T["xs", c] = xs
 
         def banks(c):
@@ -127,20 +111,20 @@ def tile_hyperbolicmlr_t_kernel(tc, x, a, p, out):
 
         def transp(c):
             for h, m in banks(c):
-                pt = ps_t.tile([P, 2, 2 * m, P], BF16, name="pt")
-                for s in range(2 * m):
-                    for v in range(2):
-                        nc.tensor.transpose(pt[:, v, s, :], T["xs", c][:, 4 * h + s, v * P:(v + 1) * P], ident_b[:])
+                pt = ps_t.tile([P, m * KB, P], BF16, name="pt")
+                for jj in range(m):
+                    for t in range(KB):
+                        nc.tensor.transpose(pt[:, jj * KB + t, :], T["xs", c][:, 2 * h + jj, t * P:(t + 1) * P], ident_b[:])
                 T["pt", c, h] = pt
 
         def evac(c, on_vector):
             if ("gx", c) not in T:
-                T["gx", c] = work3.tile([P, SIZES[c] * P, KB], BF16, name="gx", align_bytes=64)
+                T["gx", c] = work3.tile([P, SIZES[c], P, KB], BF16, name="gx", align_bytes=64)
             for h, m in banks(c):
                 if evac_on_vector(c, h) != on_vector:
                     continue
-                src = T["pt", c, h][:].rearrange("k v s (r u) -> k (s r) v u", u=2)
-                dst = T["gx", c][:, 2 * h * P:(2 * h + m) * P, :].rearrange("k c (v u) -> k c v u", u=2)
+                src = T["pt", c, h][:].rearrange("k (j t) r -> k j r t", j=m)
+                dst = T["gx", c][:, 2 * h:2 * h + m, :, :]
                 if on_vector:
                     nc.vector.tensor_copy(out=dst, in_=src)
                 else:
@@ -150,7 +134,7 @@ def tile_hyperbolicmlr_t_kernel(tc, x, a, p, out):
             n = SIZES[c]
             codes = work.tile([P, n * P], U32, name="codes", align_bytes=64)
             scales = work.tile([P, n * P], U8, name="scales", align_bytes=64)
-            nc.vector.quantize_mx(out=codes[:].bitcast(FP8X4), scales=scales[:], in_=T["gx", c][:].rearrange("k c t -> k (c t)"))
+            nc.vector.quantize_mx(out=codes[:].bitcast(FP8X4), scales=scales[:], in_=T["gx", c][:].rearrange("k j r t -> k (j r t)"))
             T["codes", c] = codes
             T["scales", c] = scales
 
@@ -173,23 +157,37 @@ def tile_hyperbolicmlr_t_kernel(tc, x, a, p, out):
             T["pu", c] = pu
             T["pv", c] = pv
 
-        def step3(c):
+        def pieces(c):
+            n = SIZES[c]
+            return [slice(i, min(i + 2, n)) for i in range(0, n, 2)]
+
+        def step3_ga(c):
             n = SIZES[c]
             mh = keep.tile([P, n, P], F32, name="mh%d" % c)
-            ee = work.tile([P, n, P], F32, name="ee")
-            va = work.tile([P, n, P], F32, name="va")
-            th = keep.tile([P, n, P], F32, name="th%d" % c)
             hb = T["hb", c]
             for j in reversed(range(n)):
                 nc.vector.scalar_tensor_tensor(out=mh[:, j, :], in0=T["pu", c][:, j, :], scalar=hb[:, j:j + 1], in1=ngam, op0=ALU.subtract, op1=ALU.mult)
+            T["mh", c] = mh
+
+        def step3_mid(c):
+            n = SIZES[c]
+            mh = T["mh", c]
+            hb = T["hb", c]
+            ee = work.tile([P, n, P], F32, name="ee")
+            va = work.tile([P, n, P], F32, name="va")
             for j in range(n):
                 nc.vector.scalar_tensor_tensor(out=ee[:, j, :], in0=nbet, scalar=hb[:, j:j + 1], in1=T["pu", c][:, j, :], op0=ALU.add, op1=ALU.subtract)
             nc.vector.tensor_tensor(out=va[:], in0=T["pv", c][:], in1=na2.unsqueeze(1).to_broadcast([P, n, P]), op=ALU.mult)
+            for s in pieces(c):
+                nc.gpsimd.tensor_tensor(out=mh[:, s, :], in0=mh[:, s, :], in1=va[:, s, :], op=ALU.add)
             nc.vector.scalar_tensor_tensor(out=ee[:], in0=ee[:], scalar=0.0, in1=ee[:], op0=ALU.max, op1=ALU.add)
-            nc.vector.tensor_tensor(out=mh[:], in0=mh[:], in1=va[:], op=ALU.add)
+            T["ee", c] = ee
+
+        def step3_th(c):
+            n = SIZES[c]
+            th = keep.tile([P, n, P], F32, name="th%d" % c)
             for j in range(n):
-                nc.vector.scalar_tensor_tensor(out=th[:, j, :], in0=bet, scalar=T["omx", c][:, j:j + 1], in1=ee[:, j, :], op0=ALU.mult, op1=ALU.add)
-            T["mh", c] = mh
+                nc.vector.scalar_tensor_tensor(out=th[:, j, :], in0=bet, scalar=T["omx", c][:, j:j + 1], in1=T["ee", c][:, j, :], op0=ALU.mult, op1=ALU.add)
             T["th", c] = th
 
         def squares(c):
@@ -202,7 +200,8 @@ def tile_hyperbolicmlr_t_kernel(tc, x, a, p, out):
             T["st", c] = st
 
         def sumsq(c):
-            nc.vector.tensor_tensor(out=T["sn", c][:], in0=T["sn", c][:], in1=T["st", c][:], op=ALU.add)
+            for s in pieces(c):
+                nc.gpsimd.tensor_tensor(out=T["sn", c][:, s, :], in0=T["sn", c][:, s, :], in1=T["st", c][:, s, :], op=ALU.add)
 
         def hypot(c):
             nc.scalar.activation(out=T["sn", c][:], in_=T["sn", c][:], func=ACT.Sqrt)
@@ -222,15 +221,6 @@ def tile_hyperbolicmlr_t_kernel(tc, x, a, p, out):
         make_identity(nc, ident_b[:])
         ident_f = const.tile([P, P], F32)
         make_identity(nc, ident_f[:])
-
-        rsel = const.tile([P, HP], F32)
-        nc.vector.reduce_sum(out=rsel[:], in_=ident_f[:].rearrange("i (r u) -> i r u", u=2), axis=AX.X)
-        pair = const.tile([P, HP, 2], F32)
-        nc.vector.tensor_copy(out=pair[:], in_=rsel[:].unsqueeze(2).to_broadcast([P, HP, 2]))
-        sel = const.tile([P, 2, P], F32)
-        nc.vector.memset(sel[:], 0.0)
-        for l in range(2):
-            nc.vector.tensor_copy(out=sel[:, l, l * HP:(l + 1) * HP], in_=rsel[:])
 
         sums = const.tile([P, 2], F32)
         an = const.tile([P, 1], F32)
@@ -254,8 +244,7 @@ def tile_hyperbolicmlr_t_kernel(tc, x, a, p, out):
                 for t in range(KB):
                     nc.tensor.transpose(pwt[:, w * KB + t, :], src[:, t * P:(t + 1) * P], ident_b[:])
             gw = const.tile([P, 2, P, KB], BF16, align_bytes=64)
-            for w in range(2):
-                nc.vector.tensor_copy(out=gw[:, w, :, :].rearrange("k c (v u) -> k c v u", u=2), in_=pwt[:, w * KB:(w + 1) * KB, :].rearrange("k (u v) c -> k c v u", u=2))
+            nc.vector.tensor_copy(out=gw[:], in_=pwt[:].rearrange("k (w t) c -> k w c t", w=2))
             prod = const.tile([P, D], F32)
             nc.vector.tensor_tensor(out=prod[:], in0=pw[:], in1=aw[:], op=ALU.mult)
             nc.vector.quantize_mx(out=w_codes[:].bitcast(FP8X4), scales=w_scales[:], in_=gw[:].rearrange("k w c t -> k (w c t)"))
@@ -278,40 +267,42 @@ def tile_hyperbolicmlr_t_kernel(tc, x, a, p, out):
             nc.vector.tensor_copy(out=ctile[:], in_=pc[:])
 
         nh = 0
-        for k in range(-6, NCH + 3):
-            if ok(k + 6 + PRE):
-                load(k + 6 + PRE)
+        for k in range(-5, NCH + 3):
+            if ok(k + 5 + PRE):
+                load(k + 5 + PRE)
             if ok(k + 3):
                 recip(k + 3)
             if ok(k + 1):
                 quant(k + 1)
+                mx(k + 1)
             if ok(k + 3):
                 factor(k + 3)
             if ok(k - 2):
                 sumsq(k - 2)
+            if ok(k):
+                step3_ga(k)
             if ok(k + 3):
                 scale(k + 3)
                 transp(k + 3)
             if k == -3:
                 setup_rest()
-            if ok(k + 4):
-                root(k + 4)
             if ok(k + 2):
                 evac(k + 2, False)
-            if ok(k + 6):
-                norms(k + 6)
-                rowsums(k + 6)
+            if ok(k + 5):
+                norms(k + 5)
+            if ok(k):
+                step3_mid(k)
+            if ok(k + 2):
+                evac(k + 2, True)
             if ok(k + 5):
                 floor_n2(k + 5)
             if ok(k):
-                step3(k)
-            if ok(k + 1):
-                mx(k + 1)
+                step3_th(k)
             if ok(k - 1):
                 squares(k - 1)
-            if ok(k + 2):
-                evac(k + 2, True)
-            if k == -6:
+            if ok(k + 4):
+                root(k + 4)
+            if k == -5:
                 setup_scalar()
             if k >= HY_START:
                 for i in range(HY_PER):

@@ -30,7 +30,7 @@ LEAD = 2
 
 
 def evac_on_vector(c, h):
-    return c < 5 or (h == 1 and c % 2 == 0)
+    return c < 5 or h == 1
 
 
 def tile_hyperbolicmlr_t_kernel(tc, x, a, p, out):
@@ -157,37 +157,23 @@ def tile_hyperbolicmlr_t_kernel(tc, x, a, p, out):
             T["pu", c] = pu
             T["pv", c] = pv
 
-        def pieces(c):
-            n = SIZES[c]
-            return [slice(i, min(i + 2, n)) for i in range(0, n, 2)]
-
-        def step3_ga(c):
+        def step3(c):
             n = SIZES[c]
             mh = keep.tile([P, n, P], F32, name="mh%d" % c)
+            ee = work.tile([P, n, P], F32, name="ee")
+            va = work.tile([P, n, P], F32, name="va")
+            th = keep.tile([P, n, P], F32, name="th%d" % c)
             hb = T["hb", c]
             for j in reversed(range(n)):
                 nc.vector.scalar_tensor_tensor(out=mh[:, j, :], in0=T["pu", c][:, j, :], scalar=hb[:, j:j + 1], in1=ngam, op0=ALU.subtract, op1=ALU.mult)
-            T["mh", c] = mh
-
-        def step3_mid(c):
-            n = SIZES[c]
-            mh = T["mh", c]
-            hb = T["hb", c]
-            ee = work.tile([P, n, P], F32, name="ee")
-            va = work.tile([P, n, P], F32, name="va")
             for j in range(n):
                 nc.vector.scalar_tensor_tensor(out=ee[:, j, :], in0=nbet, scalar=hb[:, j:j + 1], in1=T["pu", c][:, j, :], op0=ALU.add, op1=ALU.subtract)
             nc.vector.tensor_tensor(out=va[:], in0=T["pv", c][:], in1=na2.unsqueeze(1).to_broadcast([P, n, P]), op=ALU.mult)
-            for s in pieces(c):
-                nc.gpsimd.tensor_tensor(out=mh[:, s, :], in0=mh[:, s, :], in1=va[:, s, :], op=ALU.add)
             nc.vector.scalar_tensor_tensor(out=ee[:], in0=ee[:], scalar=0.0, in1=ee[:], op0=ALU.max, op1=ALU.add)
-            T["ee", c] = ee
-
-        def step3_th(c):
-            n = SIZES[c]
-            th = keep.tile([P, n, P], F32, name="th%d" % c)
+            nc.vector.tensor_tensor(out=mh[:], in0=mh[:], in1=va[:], op=ALU.add)
             for j in range(n):
-                nc.vector.scalar_tensor_tensor(out=th[:, j, :], in0=bet, scalar=T["omx", c][:, j:j + 1], in1=T["ee", c][:, j, :], op0=ALU.mult, op1=ALU.add)
+                nc.vector.scalar_tensor_tensor(out=th[:, j, :], in0=bet, scalar=T["omx", c][:, j:j + 1], in1=ee[:, j, :], op0=ALU.mult, op1=ALU.add)
+            T["mh", c] = mh
             T["th", c] = th
 
         def squares(c):
@@ -200,8 +186,7 @@ def tile_hyperbolicmlr_t_kernel(tc, x, a, p, out):
             T["st", c] = st
 
         def sumsq(c):
-            for s in pieces(c):
-                nc.gpsimd.tensor_tensor(out=T["sn", c][:, s, :], in0=T["sn", c][:, s, :], in1=T["st", c][:, s, :], op=ALU.add)
+            nc.vector.tensor_tensor(out=T["sn", c][:], in0=T["sn", c][:], in1=T["st", c][:], op=ALU.add)
 
         def hypot(c):
             nc.scalar.activation(out=T["sn", c][:], in_=T["sn", c][:], func=ACT.Sqrt)
@@ -279,8 +264,6 @@ def tile_hyperbolicmlr_t_kernel(tc, x, a, p, out):
                 factor(k + 3)
             if ok(k - 2):
                 sumsq(k - 2)
-            if ok(k):
-                step3_ga(k)
             if ok(k + 3):
                 scale(k + 3)
                 transp(k + 3)
@@ -291,15 +274,13 @@ def tile_hyperbolicmlr_t_kernel(tc, x, a, p, out):
             if ok(k + 5):
                 norms(k + 5)
             if ok(k):
-                step3_mid(k)
+                step3(k)
+            if ok(k - 1):
+                squares(k - 1)
             if ok(k + 2):
                 evac(k + 2, True)
             if ok(k + 5):
                 floor_n2(k + 5)
-            if ok(k):
-                step3_th(k)
-            if ok(k - 1):
-                squares(k - 1)
             if ok(k + 4):
                 root(k + 4)
             if k == -5:

@@ -30,7 +30,7 @@ LEAD = 2
 
 
 def evac_on_vector(c, h):
-    return c < 5 or h == 1
+    return c < 5
 
 
 def tile_hyperbolicmlr_t_kernel(tc, x, a, p, out):

@@ -30,7 +30,7 @@ LEAD = 2
 
 
 def evac_on_vector(c, h):
-    return c < 5
+    return c < 4
 
 
 def tile_hyperbolicmlr_t_kernel(tc, x, a, p, out):
@@ -42,7 +42,7 @@ def tile_hyperbolicmlr_t_kernel(tc, x, a, p, out):
         const = ctx.enter_context(tc.tile_pool(name="const", bufs=1))
         keep = ctx.enter_context(tc.tile_pool(name="keep", bufs=1))
         xin = ctx.enter_context(tc.tile_pool(name="xin", bufs=8))
-        small = ctx.enter_context(tc.tile_pool(name="small", bufs=8))
+        small = ctx.enter_context(tc.tile_pool(name="small", bufs=9))
         work = ctx.enter_context(tc.tile_pool(name="work", bufs=2))
         work3 = ctx.enter_context(tc.tile_pool(name="work3", bufs=3))
         ps_t = ctx.enter_context(tc.psum_pool(name="ps_t", bufs=4))
@@ -72,7 +72,7 @@ def tile_hyperbolicmlr_t_kernel(tc, x, a, p, out):
         def floor_n2(c):
             n = SIZES[c]
             n2c = small.tile([P, n], F32, name="n2c")
-            nc.vector.tensor_scalar(out=n2c[:], in0=T["n2", c][:], scalar1=1e-30, scalar2=None, op0=ALU.max)
+            nc.gpsimd.tensor_scalar(out=n2c[:], in0=T["n2", c][:], scalar1=1e-30, scalar2=None, op0=ALU.max)
             T["n2c", c] = n2c
             x2 = small.tile([P, n], F32, name="x2")
             nc.gpsimd.tensor_scalar(out=x2[:], in0=T["n2", c][:], scalar1=MAXN * MAXN, scalar2=None, op0=ALU.min)
@@ -95,7 +95,7 @@ def tile_hyperbolicmlr_t_kernel(tc, x, a, p, out):
 
         def factor(c):
             sc = small.tile([P, SIZES[c]], F32, name="sc")
-            nc.vector.tensor_scalar(out=sc[:], in0=T["rn", c][:], scalar1=MAXN, scalar2=1.0, op0=ALU.mult, op1=ALU.min)
+            nc.gpsimd.tensor_scalar(out=sc[:], in0=T["rn", c][:], scalar1=MAXN, scalar2=1.0, op0=ALU.mult, op1=ALU.min)
             T["sc", c] = sc
 
         def scale(c):
@@ -252,16 +252,15 @@ def tile_hyperbolicmlr_t_kernel(tc, x, a, p, out):
             nc.vector.tensor_copy(out=ctile[:], in_=pc[:])
 
         nh = 0
-        for k in range(-5, NCH + 3):
-            if ok(k + 5 + PRE):
+        for k in range(-6, NCH + 3):
+            if k >= -5 and ok(k + 5 + PRE):
                 load(k + 5 + PRE)
-            if ok(k + 3):
-                recip(k + 3)
+            if ok(k + 4):
+                recip(k + 4)
+                factor(k + 4)
             if ok(k + 1):
                 quant(k + 1)
                 mx(k + 1)
-            if ok(k + 3):
-                factor(k + 3)
             if ok(k - 2):
                 sumsq(k - 2)
             if ok(k + 3):
@@ -271,19 +270,19 @@ def tile_hyperbolicmlr_t_kernel(tc, x, a, p, out):
                 setup_rest()
             if ok(k + 2):
                 evac(k + 2, False)
-            if ok(k + 5):
-                norms(k + 5)
+            if ok(k + 6):
+                norms(k + 6)
             if ok(k):
                 step3(k)
             if ok(k - 1):
                 squares(k - 1)
             if ok(k + 2):
                 evac(k + 2, True)
+            if ok(k + 6):
+                floor_n2(k + 6)
             if ok(k + 5):
-                floor_n2(k + 5)
-            if ok(k + 4):
-                root(k + 4)
-            if k == -5:
+                root(k + 5)
+            if k == -6:
                 setup_scalar()
             if k >= HY_START:
                 for i in range(HY_PER):

@@ -19,14 +19,14 @@ KB = D // P
 MAXN = 1.0 - 1e-5
 FLOPS = 2 * B * D * 2 * C
 
-SIZES = (1, 1, 2) + (4,) * 15
+SIZES = (1, 1, 2) + (4,) * 13 + (2,) * 4
 NCH = len(SIZES)
 STARTS = tuple(sum(SIZES[:i]) for i in range(NCH))
 CMAX = max(SIZES)
 PRE = 5
 HY_START = 13
-HY_PER = 3
-LEAD = 2
+HY_PER = 4
+LEAD = 3
 
 
 def evac_on_vector(c, h):

@@ -10,27 +10,23 @@ U8 = mybir.dt.uint8
 FP8X4 = mybir.dt.float8_e4m3fn_x4
 ALU = mybir.AluOpType
 ACT = mybir.ActivationFunctionType
-AX = mybir.AxisListType
 
 B, D, C = 8192, 512, 128
 P = 128
 NT = B // P
-KB = D // P
+KW = D // 2 // P
 MAXN = 1.0 - 1e-5
 FLOPS = 2 * B * D * 2 * C
 
-SIZES = (1, 1, 2) + (4,) * 13 + (2,) * 4
+SIZES = (1, 1, 2) + (4,) * 14 + (2, 2)
 NCH = len(SIZES)
 STARTS = tuple(sum(SIZES[:i]) for i in range(NCH))
-CMAX = max(SIZES)
 PRE = 5
-HY_START = 13
-HY_PER = 4
-LEAD = 3
 
 
-def evac_on_vector(c, h):
-    return c < 4
+def norms_on_vector(c):
+    n = SIZES[c]
+    return 0 if n == 1 else 1 if n == 2 else 1 + c % 2
 
 
 def tile_hyperbolicmlr_t_kernel(tc, x, a, p, out):
@@ -45,9 +41,11 @@ def tile_hyperbolicmlr_t_kernel(tc, x, a, p, out):
         small = ctx.enter_context(tc.tile_pool(name="small", bufs=9))
         work = ctx.enter_context(tc.tile_pool(name="work", bufs=2))
         work3 = ctx.enter_context(tc.tile_pool(name="work3", bufs=3))
-        ps_t = ctx.enter_context(tc.psum_pool(name="ps_t", bufs=4))
+        stage = ctx.enter_context(tc.tile_pool(name="stage", bufs=8))
+        ps_t = ctx.enter_context(tc.psum_pool(name="ps_t", bufs=3))
         ps_u = ctx.enter_context(tc.psum_pool(name="ps_u", bufs=2))
         ps_v = ctx.enter_context(tc.psum_pool(name="ps_v", bufs=2))
+        ps_s = ctx.enter_context(tc.psum_pool(name="ps_s", bufs=1))
         ctx.enter_context(tc.manual_schedule())
 
         T = {}
@@ -61,135 +59,136 @@ def tile_hyperbolicmlr_t_kernel(tc, x, a, p, out):
             nc.sync.dma_start(out=xr[:], in_=xv[:, STARTS[c]:STARTS[c] + n, :])
             T["xr", c] = xr
 
-        def norms(c):
+        def norms_v(c):
             n = SIZES[c]
-            n2 = small.tile([P, n], F32, name="n2")
-            for j in range(n):
-                junk = work.tile([P, D], BF16, name="junk")
-                nc.scalar.activation(out=junk[:], in_=T["xr", c][:, j, :], func=ACT.Square, accum_out=n2[:, j:j + 1])
-            T["n2", c] = n2
+            T["n2", c] = small.tile([P, n], F32, name="n2")
+            for j in range(norms_on_vector(c)):
+                xj = T["xr", c][:, j, :]
+                junk = work.tile([P, D], BF16, name="junk_v")
+                nc.vector.scalar_tensor_tensor(out=junk[:], in0=xj, scalar=1.0, in1=xj, op0=ALU.mult, op1=ALU.mult, accum_out=T["n2", c][:, j:j + 1])
 
-        def floor_n2(c):
-            n = SIZES[c]
-            n2c = small.tile([P, n], F32, name="n2c")
-            nc.gpsimd.tensor_scalar(out=n2c[:], in0=T["n2", c][:], scalar1=1e-30, scalar2=None, op0=ALU.max)
-            T["n2c", c] = n2c
-            x2 = small.tile([P, n], F32, name="x2")
-            nc.gpsimd.tensor_scalar(out=x2[:], in0=T["n2", c][:], scalar1=MAXN * MAXN, scalar2=None, op0=ALU.min)
-            hb = small.tile([P, n], F32, name="hb")
-            nc.gpsimd.tensor_scalar(out=hb[:], in0=x2[:], scalar1=0.5, scalar2=0.5, op0=ALU.mult, op1=ALU.add)
-            omx = small.tile([P, n], F32, name="omx")
-            nc.gpsimd.tensor_scalar(out=omx[:], in0=x2[:], scalar1=-1.0, scalar2=1.0, op0=ALU.mult, op1=ALU.add)
-            T["hb", c] = hb
-            T["omx", c] = omx
+        def norms_s(c):
+            for j in range(norms_on_vector(c), SIZES[c]):
+                junk = work.tile([P, D], BF16, name="junk_s")
+                nc.scalar.activation(out=junk[:], in_=T["xr", c][:, j, :], func=ACT.Square, accum_out=T["n2", c][:, j:j + 1])
 
-        def root(c):
-            nr = small.tile([P, SIZES[c]], F32, name="nr")
-            nc.scalar.activation(out=nr[:], in_=T["n2c", c][:], func=ACT.Sqrt)
-            T["nr", c] = nr
-
-        def recip(c):
+        def inv_norm(c):
             rn = small.tile([P, SIZES[c]], F32, name="rn")
-            nc.vector.reciprocal(out=rn[:], in_=T["nr", c][:])
+            nc.scalar.activation(out=rn[:], in_=T["n2", c][:], func=ACT.Abs_reciprocal_sqrt)
             T["rn", c] = rn
 
         def factor(c):
-            sc = small.tile([P, SIZES[c]], F32, name="sc")
-            nc.gpsimd.tensor_scalar(out=sc[:], in0=T["rn", c][:], scalar1=MAXN, scalar2=1.0, op0=ALU.mult, op1=ALU.min)
-            T["sc", c] = sc
-
-        def scale(c):
             n = SIZES[c]
-            xs = work.tile([P, n, D], BF16, name="xs")
-            for j in range(n):
-                nc.vector.tensor_scalar(out=xs[:, j, :], in0=T["xr", c][:, j, :], scalar1=T["sc", c][:, j:j + 1], scalar2=None, op0=ALU.mult)
-            T["xs", c] = xs
+            sc = small.tile([P, n], F32, name="sc")
+            nc.gpsimd.tensor_scalar(out=sc[:], in0=T["rn", c][:], scalar1=MAXN, scalar2=1.0, op0=ALU.mult, op1=ALU.min)
+            s1 = small.tile([P, n], F32, name="s1")
+            nc.gpsimd.tensor_scalar(out=s1[:], in0=T["n2", c][:], scalar1=MAXN * MAXN, scalar2=1.0, op0=ALU.min, op1=ALU.add)
+            T["sc", c] = sc
+            T["s1", c] = s1
 
-        def banks(c):
+        def halves(c):
             n = SIZES[c]
             return [(h, min(2, n - 2 * h)) for h in range((n + 1) // 2)]
 
-        def transp(c):
-            for h, m in banks(c):
-                pt = ps_t.tile([P, m * KB, P], BF16, name="pt")
-                for jj in range(m):
-                    for t in range(KB):
-                        nc.tensor.transpose(pt[:, jj * KB + t, :], T["xs", c][:, 2 * h + jj, t * P:(t + 1) * P], ident_b[:])
-                T["pt", c, h] = pt
+        def scale(c, h, m):
+            if h == 0:
+                T["xs", c] = work.tile([P, SIZES[c], D], BF16, name="xs")
+            for j in range(2 * h, 2 * h + m):
+                nc.vector.tensor_scalar(out=T["xs", c][:, j, :], in0=T["xr", c][:, j, :], scalar1=T["sc", c][:, j:j + 1], scalar2=None, op0=ALU.mult)
 
-        def evac(c, on_vector):
-            if ("gx", c) not in T:
-                T["gx", c] = work3.tile([P, SIZES[c], P, KB], BF16, name="gx", align_bytes=64)
-            for h, m in banks(c):
-                if evac_on_vector(c, h) != on_vector:
-                    continue
-                src = T["pt", c, h][:].rearrange("k (j t) r -> k j r t", j=m)
-                dst = T["gx", c][:, 2 * h:2 * h + m, :, :]
-                if on_vector:
-                    nc.vector.tensor_copy(out=dst, in_=src)
-                else:
-                    nc.scalar.copy(out=dst, in_=src)
+        def transp(c, h, m):
+            pt = ps_t.tile([P, m, KW, P], F32, name="pt")
+            for jj in range(m):
+                words = T["xs", c][:, 2 * h + jj, :].bitcast(F32)
+                for w in range(KW):
+                    nc.tensor.transpose(pt[:, jj, w, :], words[:, w * P:(w + 1) * P], ident[:])
+            T["pt", c, h] = pt
+
+        def evac(c, h, m):
+            if h == 0:
+                T["gx", c] = work3.tile([P, SIZES[c] * P * 4], BF16, name="gx", align_bytes=64)
+            dst = T["gx", c][:].bitcast(F32).rearrange("k (j r w) -> k j r w", r=P, w=KW)[:, 2 * h:2 * h + m, :, :]
+            nc.scalar.copy(out=dst, in_=T["pt", c, h][:].rearrange("k j w r -> k j r w"))
 
         def quant(c):
             n = SIZES[c]
             codes = work.tile([P, n * P], U32, name="codes", align_bytes=64)
             scales = work.tile([P, n * P], U8, name="scales", align_bytes=64)
-            nc.vector.quantize_mx(out=codes[:].bitcast(FP8X4), scales=scales[:], in_=T["gx", c][:].rearrange("k j r t -> k (j r t)"))
+            nc.vector.quantize_mx(out=codes[:].bitcast(FP8X4), scales=scales[:], in_=T["gx", c][:])
             T["codes", c] = codes
             T["scales", c] = scales
 
         def mx(c):
             n = SIZES[c]
-            pu = ps_u.tile([P, n, P], F32, name="pu")
-            pv = ps_v.tile([P, n, P], F32, name="pv")
-            for j in range(n):
-                cols = slice(j * P, (j + 1) * P)
-                for w, dstp in enumerate((pu, pv)):
-                    nc.tensor.matmul_mx(
-                        out=dstp[:, j, :],
-                        lhsT=T["codes", c][:, cols].bitcast(FP8X4),
-                        lhsT_scale=T["scales", c][:, cols],
-                        rhs=w_codes[:, w * P:(w + 1) * P].bitcast(FP8X4),
-                        rhs_scale=w_scales[:, w * P:(w + 1) * P],
-                        start=True,
-                        stop=True,
-                    )
-            T["pu", c] = pu
-            T["pv", c] = pv
+            for i, (nm, pool) in enumerate((("pu", ps_u), ("pv", ps_v))):
+                acc = pool.tile([P, n * P], F32, name=nm)
+                nc.tensor.matmul_mx(
+                    out=acc[:],
+                    lhsT=w_codes[:, i * P:(i + 1) * P].bitcast(FP8X4),
+                    lhsT_scale=w_scales[:, i * P:(i + 1) * P],
+                    rhs=T["codes", c][:].bitcast(FP8X4),
+                    rhs_scale=T["scales", c][:],
+                    start=True,
+                    stop=True,
+                )
+                T[nm, c] = acc
 
-        def step3(c):
+        def spread(c):
             n = SIZES[c]
-            mh = keep.tile([P, n, P], F32, name="mh%d" % c)
-            ee = work.tile([P, n, P], F32, name="ee")
-            va = work.tile([P, n, P], F32, name="va")
-            th = keep.tile([P, n, P], F32, name="th%d" % c)
-            hb = T["hb", c]
-            for j in reversed(range(n)):
-                nc.vector.scalar_tensor_tensor(out=mh[:, j, :], in0=T["pu", c][:, j, :], scalar=hb[:, j:j + 1], in1=ngam, op0=ALU.subtract, op1=ALU.mult)
+            pb = ps_s.tile([P, n, P], F32, name="pb")
             for j in range(n):
-                nc.vector.scalar_tensor_tensor(out=ee[:, j, :], in0=nbet, scalar=hb[:, j:j + 1], in1=T["pu", c][:, j, :], op0=ALU.add, op1=ALU.subtract)
-            nc.vector.tensor_tensor(out=va[:], in0=T["pv", c][:], in1=na2.unsqueeze(1).to_broadcast([P, n, P]), op=ALU.mult)
-            nc.vector.scalar_tensor_tensor(out=ee[:], in0=ee[:], scalar=0.0, in1=ee[:], op0=ALU.max, op1=ALU.add)
-            nc.vector.tensor_tensor(out=mh[:], in0=mh[:], in1=va[:], op=ALU.add)
-            for j in range(n):
-                nc.vector.scalar_tensor_tensor(out=th[:, j, :], in0=bet, scalar=T["omx", c][:, j:j + 1], in1=ee[:, j, :], op0=ALU.mult, op1=ALU.add)
-            T["mh", c] = mh
-            T["th", c] = th
+                nc.tensor.transpose(pb[:, j, :], T["s1", c][:, j:j + 1].to_broadcast([P, P]), ident[:])
+            T["pb", c] = pb
 
-        def squares(c):
-            n = SIZES[c]
-            sn = keep.tile([P, n, P], F32, name="sn%d" % c)
-            nc.scalar.activation(out=sn[:], in_=T["mh", c][:], func=ACT.Square)
-            st = work3.tile([P, n, P], F32, name="st")
-            nc.scalar.activation(out=st[:], in_=T["th", c][:], func=ACT.Square)
-            T["sn", c] = sn
-            T["st", c] = st
+        def copy_s1(c):
+            sb = work3.tile([P, SIZES[c] * P], F32, name="sb")
+            nc.scalar.copy(out=sb[:], in_=T["pb", c][:].rearrange("k j r -> k (j r)"))
+            T["sb", c] = sb
 
-        def sumsq(c):
-            nc.vector.tensor_tensor(out=T["sn", c][:], in0=T["sn", c][:], in1=T["st", c][:], op=ALU.add)
+        def form_a(c):
+            ta = work.tile([P, SIZES[c] * P], F32, name="ta")
+            nc.vector.scalar_tensor_tensor(out=ta[:], in0=T["pu", c][:], scalar=-2.0, in1=T["sb", c][:], op0=ALU.mult, op1=ALU.add)
+            T["ta", c] = ta
 
-        def hypot(c):
-            nc.scalar.activation(out=T["sn", c][:], in_=T["sn", c][:], func=ACT.Sqrt)
+        def form_r(c):
+            tt = work3.tile([P, SIZES[c] * P], F32, name="tt")
+            nc.vector.tensor_scalar(out=tt[:], in0=T["ta", c][:], scalar1=beta[:], scalar2=None, op0=ALU.max)
+            T["tt", c] = tt
+
+        def form_m(c):
+            tm = keep.tile([P, SIZES[c] * P], F32, name="tm%d" % c)
+            nc.vector.scalar_tensor_tensor(out=tm[:], in0=T["ta", c][:], scalar=fcol[:], in1=T["pv", c][:], op0=ALU.mult, op1=ALU.add)
+            T["tm", c] = tm
+
+        def form_t(c):
+            tt = T["tt", c]
+            nc.vector.scalar_tensor_tensor(out=tt[:], in0=T["sb", c][:], scalar=nhb[:], in1=tt[:], op0=ALU.mult, op1=ALU.add)
+
+        def square_t(c):
+            tt = T["tt", c]
+            nc.scalar.activation(out=tt[:], in_=tt[:], func=ACT.Square)
+
+        def inv_t(c):
+            tt = T["tt", c]
+            nc.scalar.activation(out=tt[:], in_=tt[:], func=ACT.Abs_reciprocal_sqrt)
+
+        def form_z(c):
+            tm = T["tm", c]
+            nc.vector.scalar_tensor_tensor(out=tm[:], in0=tm[:], scalar=ecol[:], in1=T["tt", c][:], op0=ALU.mult, op1=ALU.mult)
+
+        def square_z(c):
+            sq = keep.tile([P, SIZES[c] * P], F32, name="sq%d" % c)
+            nc.scalar.activation(out=sq[:], in_=T["tm", c][:], func=ACT.Square)
+            T["sq", c] = sq
+
+        def inv_h(c):
+            tg = work3.tile([P, SIZES[c] * P], F32, name="tg")
+            nc.scalar.activation(out=tg[:], in_=T["sq", c][:], func=ACT.Abs_reciprocal_sqrt, bias=one1[:])
+            T["tg", c] = tg
+
+        def form_h(c):
+            sq = T["sq", c]
+            nc.vector.scalar_tensor_tensor(out=sq[:], in0=sq[:], scalar=1.0, in1=T["tg", c][:], op0=ALU.add, op1=ALU.mult)
 
         load(0)
         pw = const.tile([P, D], BF16)
@@ -201,19 +200,16 @@ def tile_hyperbolicmlr_t_kernel(tc, x, a, p, out):
         one1 = const.tile([P, 1], F32)
         nc.vector.memset(one1[:], 1.0)
         warm = const.tile([P, 1], F32)
-        nc.scalar.activation(out=warm[:], in_=one1[:], func=ACT.Sqrt)
-        ident_b = const.tile([P, P], BF16)
-        make_identity(nc, ident_b[:])
-        ident_f = const.tile([P, P], F32)
-        make_identity(nc, ident_f[:])
+        nc.scalar.activation(out=warm[:], in_=one1[:], func=ACT.Abs_reciprocal_sqrt)
+        ident = const.tile([P, P], F32)
+        make_identity(nc, ident[:])
 
+        beta = const.tile([P, 1], F32)
+        nhb = const.tile([P, 1], F32)
+        fcol = const.tile([P, 1], F32)
+        ecol = const.tile([P, 1], F32)
         sums = const.tile([P, 2], F32)
-        an = const.tile([P, 1], F32)
-        ctile = const.tile([P, 4, P], F32)
-        na2 = ctile[:, 0, :]
-        ngam = ctile[:, 1, :]
-        bet = ctile[:, 2, :]
-        nbet = ctile[:, 3, :]
+        ran = const.tile([P, 1], F32)
         w_codes = const.tile([P, 2 * P], U32, align_bytes=64)
         w_scales = const.tile([P, 2 * P], U8, align_bytes=64)
 
@@ -221,84 +217,90 @@ def tile_hyperbolicmlr_t_kernel(tc, x, a, p, out):
             junk_w = const.tile([P, D], BF16)
             nc.scalar.activation(out=junk_w[:], in_=pw[:], func=ACT.Square, accum_out=sums[:, 0:1])
             nc.scalar.activation(out=junk_w[:], in_=aw[:], func=ACT.Square, accum_out=sums[:, 1:2])
-            nc.scalar.activation(out=an[:], in_=sums[:, 1:2], func=ACT.Sqrt)
+            nc.scalar.activation(out=ran[:], in_=sums[:, 1:2], func=ACT.Abs_reciprocal_sqrt)
 
         def setup_rest():
-            pwt = ps_t.tile([P, 2 * KB, P], BF16, name="pt")
-            for w, src in enumerate((pw, aw)):
-                for t in range(KB):
-                    nc.tensor.transpose(pwt[:, w * KB + t, :], src[:, t * P:(t + 1) * P], ident_b[:])
-            gw = const.tile([P, 2, P, KB], BF16, align_bytes=64)
-            nc.vector.tensor_copy(out=gw[:], in_=pwt[:].rearrange("k (w t) c -> k w c t", w=2))
-            prod = const.tile([P, D], F32)
-            nc.vector.tensor_tensor(out=prod[:], in0=pw[:], in1=aw[:], op=ALU.mult)
-            nc.vector.quantize_mx(out=w_codes[:].bitcast(FP8X4), scales=w_scales[:], in_=gw[:].rearrange("k w c t -> k (w c t)"))
+            pwt = ps_t.tile([P, 2, KW, P], F32, name="pt")
+            for i, src in enumerate((pw, aw)):
+                words = src[:].bitcast(F32)
+                for w in range(KW):
+                    nc.tensor.transpose(pwt[:, i, w, :], words[:, w * P:(w + 1) * P], ident[:])
+            gw = const.tile([P, 2 * P * 4], BF16, align_bytes=64)
+            nc.vector.tensor_copy(out=gw[:].bitcast(F32).rearrange("k (i c w) -> k i c w", i=2, w=KW), in_=pwt[:].rearrange("k i w c -> k i c w"))
+            junk_p = const.tile([P, D], BF16)
             pa = const.tile([P, 1], F32)
-            nc.vector.reduce_sum(out=pa[:], in_=prod[:], axis=AX.X)
-            ran = const.tile([P, 1], F32)
-            nc.vector.reciprocal(out=ran[:], in_=an[:])
-            bc = const.tile([P, 1], F32)
-            nc.vector.tensor_scalar(out=bc[:], in0=sums[:, 0:1], scalar1=-1.0, scalar2=1.0, op0=ALU.mult, op1=ALU.add)
-            kc = const.tile([P, 4], F32)
-            nc.vector.tensor_scalar(out=kc[:, 0:1], in0=bc[:], scalar1=ran[:, 0:1], scalar2=-1.0, op0=ALU.mult, op1=ALU.mult)
-            nc.vector.tensor_scalar(out=kc[:, 1:2], in0=pa[:], scalar1=ran[:, 0:1], scalar2=-2.0, op0=ALU.mult, op1=ALU.mult)
-            nc.vector.tensor_scalar(out=kc[:, 2:3], in0=bc[:], scalar1=0.5, scalar2=None, op0=ALU.mult)
-            nc.vector.tensor_scalar(out=kc[:, 3:4], in0=bc[:], scalar1=-0.5, scalar2=None, op0=ALU.mult)
-            rep = const.tile([P, 4, P], F32)
-            nc.vector.tensor_copy(out=rep[:], in_=kc[:].unsqueeze(2).to_broadcast([P, 4, P]))
-            pc = ps_t.tile([P, 4, P], F32, name="pt")
-            for j in range(4):
-                nc.tensor.transpose(pc[:, j, :], rep[:, j, :], ident_f[:])
-            nc.vector.tensor_copy(out=ctile[:], in_=pc[:])
+            nc.vector.scalar_tensor_tensor(out=junk_p[:], in0=pw[:], scalar=1.0, in1=aw[:], op0=ALU.mult, op1=ALU.mult, accum_out=pa[:])
+            nc.vector.quantize_mx(out=w_codes[:].bitcast(FP8X4), scales=w_scales[:], in_=gw[:])
+            nc.vector.tensor_scalar(out=beta[:], in0=sums[:, 0:1], scalar1=-1.0, scalar2=1.0, op0=ALU.mult, op1=ALU.add)
+            safe = const.tile([P, 1], F32)
+            nc.vector.tensor_scalar(out=safe[:], in0=beta[:], scalar1=0.0, scalar2=1e-20, op0=ALU.is_equal, op1=ALU.mult)
+            nc.vector.tensor_tensor(out=safe[:], in0=safe[:], in1=beta[:], op=ALU.add)
+            rb = const.tile([P, 1], F32)
+            nc.vector.reciprocal(out=rb[:], in_=safe[:])
+            nc.vector.tensor_scalar(out=nhb[:], in0=beta[:], scalar1=-0.5, scalar2=None, op0=ALU.mult)
+            nc.vector.tensor_scalar(out=fcol[:], in0=pa[:], scalar1=rb[:], scalar2=-1.0, op0=ALU.mult, op1=ALU.mult)
+            nc.vector.tensor_scalar(out=ecol[:], in0=safe[:], scalar1=ran[:], scalar2=-1.0, op0=ALU.mult, op1=ALU.mult)
 
-        nh = 0
-        for k in range(-6, NCH + 3):
-            if k >= -5 and ok(k + 5 + PRE):
+        for k in range(-5, NCH + 4):
+            if ok(k + 5 + PRE):
                 load(k + 5 + PRE)
-            if ok(k + 4):
-                recip(k + 4)
-                factor(k + 4)
+            first = halves(k + 3)[0] if ok(k + 3) else None
+            second = halves(k + 3)[1] if ok(k + 3) and len(halves(k + 3)) > 1 else None
             if ok(k + 1):
                 quant(k + 1)
                 mx(k + 1)
-            if ok(k - 2):
-                sumsq(k - 2)
-            if ok(k + 3):
-                scale(k + 3)
-                transp(k + 3)
+                spread(k + 1)
+            if ok(k - 1):
+                square_t(k - 1)
+            if ok(k + 2):
+                evac(k + 2, *halves(k + 2)[0])
+            if ok(k - 1):
+                inv_t(k - 1)
+            if ok(k + 2) and len(halves(k + 2)) > 1:
+                evac(k + 2, *halves(k + 2)[1])
+            if ok(k + 4):
+                inv_norm(k + 4)
+                factor(k + 4)
+            if ok(k + 1):
+                copy_s1(k + 1)
+            if ok(k):
+                form_a(k)
+            if first:
+                scale(k + 3, *first)
+                transp(k + 3, *first)
+            if ok(k):
+                form_r(k)
+                form_m(k)
+            if second:
+                scale(k + 3, *second)
+                transp(k + 3, *second)
+            if ok(k):
+                form_t(k)
             if k == -3:
                 setup_rest()
-            if ok(k + 2):
-                evac(k + 2, False)
-            if ok(k + 6):
-                norms(k + 6)
-            if ok(k):
-                step3(k)
-            if ok(k - 1):
-                squares(k - 1)
-            if ok(k + 2):
-                evac(k + 2, True)
-            if ok(k + 6):
-                floor_n2(k + 6)
+            if ok(k - 2):
+                square_z(k - 2)
             if ok(k + 5):
-                root(k + 5)
-            if k == -6:
+                norms_v(k + 5)
+                norms_s(k + 5)
+            if ok(k - 2):
+                inv_h(k - 2)
+            if k == -5:
                 setup_scalar()
-            if k >= HY_START:
-                for i in range(HY_PER):
-                    if nh < NCH and nh <= k - 3:
-                        hypot(nh)
-                        nh += 1
-        while nh < NCH:
-            hypot(nh)
-            nh += 1
+            if ok(k - 1):
+                form_z(k - 1)
+            if ok(k - 3):
+                form_h(k - 3)
 
-        for c in range(NCH + LEAD):
-            if ok(c):
-                nc.vector.tensor_tensor(out=T["sn", c][:], in0=T["sn", c][:], in1=T["mh", c][:], op=ALU.add)
-                nc.scalar.activation(out=T["th", c][:], in_=T["th", c][:], func=ACT.Ln)
-                nc.scalar.activation(out=T["sn", c][:], in_=T["sn", c][:], func=ACT.Ln)
-            d = c - LEAD
-            if ok(d):
-                nc.vector.tensor_tensor(out=T["sn", d][:], in0=T["sn", d][:], in1=T["th", d][:], op=ALU.subtract)
-                nc.sync.dma_start(out=ov[:, STARTS[d]:STARTS[d] + SIZES[d], :], in_=T["sn", d][:])
+        banks = ((ps_t, "pt"), (ps_u, "pu"), (ps_v, "pv"), (ps_t, "pt"), (ps_u, "pu"), (ps_v, "pv"), (ps_t, "pt"), (ps_s, "pb"))
+        for c in range(NCH):
+            n = SIZES[c]
+            pool, nm = banks[c % len(banks)]
+            acc = pool.tile([P, n, P], F32, name=nm)
+            for j in range(n):
+                cols = slice(j * P, (j + 1) * P)
+                nc.tensor.matmul(acc[:, j, :], lhsT=T["tm", c][:, cols], rhs=ident[:], start=True, stop=False, is_transpose=True)
+                nc.tensor.matmul(acc[:, j, :], lhsT=T["sq", c][:, cols], rhs=ident[:], start=False, stop=True, is_transpose=True)
+            res = stage.tile([P, n, P], F32, name="res")
+            nc.scalar.activation(out=res[:], in_=acc[:], func=ACT.Ln)
+            nc.sync.dma_start(out=ov[:, STARTS[c]:STARTS[c] + n, :], in_=res[:])

@@ -26,7 +26,7 @@ PRE = 5
 
 def norms_on_vector(c):
     n = SIZES[c]
-    return 0 if n == 1 else 1 if n == 2 else 1 + c % 2
+    return n // 2
 
 
 def tile_hyperbolicmlr_t_kernel(tc, x, a, p, out):
@@ -182,13 +182,27 @@ def tile_hyperbolicmlr_t_kernel(tc, x, a, p, out):
             T["sq", c] = sq
 
         def inv_h(c):
-            tg = work3.tile([P, SIZES[c] * P], F32, name="tg")
+            tg = keep.tile([P, SIZES[c] * P], F32, name="tg%d" % c)
             nc.scalar.activation(out=tg[:], in_=T["sq", c][:], func=ACT.Abs_reciprocal_sqrt, bias=one1[:])
             T["tg", c] = tg
 
         def form_h(c):
             sq = T["sq", c]
             nc.vector.scalar_tensor_tensor(out=sq[:], in0=sq[:], scalar=1.0, in1=T["tg", c][:], op0=ALU.add, op1=ALU.mult)
+
+        order = list(range(3, NCH)) + [2, 1, 0]
+        banks = ((ps_t, "pt"), (ps_t, "pt"), (ps_t, "pt"), (ps_s, "pb"), (ps_u, "pu"), (ps_v, "pv"), (ps_u, "pu"), (ps_v, "pv"))
+
+        def turn(i):
+            c = order[i]
+            pool, nm = banks[i % len(banks)]
+            form_h(c)
+            acc = pool.tile([P, SIZES[c], P], F32, name=nm)
+            for j in range(SIZES[c]):
+                cols = slice(j * P, (j + 1) * P)
+                nc.tensor.matmul(acc[:, j, :], lhsT=T["tm", c][:, cols], rhs=ident[:], start=True, stop=False, is_transpose=True)
+                nc.tensor.matmul(acc[:, j, :], lhsT=T["sq", c][:, cols], rhs=ident[:], start=False, stop=True, is_transpose=True)
+            T["acc", c] = acc
 
         load(0)
         pw = const.tile([P, D], BF16)
@@ -208,15 +222,15 @@ def tile_hyperbolicmlr_t_kernel(tc, x, a, p, out):
         nhb = const.tile([P, 1], F32)
         fcol = const.tile([P, 1], F32)
         ecol = const.tile([P, 1], F32)
-        sums = const.tile([P, 2], F32)
+        sums = const.tile([P, 3], F32)
         ran = const.tile([P, 1], F32)
         w_codes = const.tile([P, 2 * P], U32, align_bytes=64)
         w_scales = const.tile([P, 2 * P], U8, align_bytes=64)
 
-        def setup_scalar():
-            junk_w = const.tile([P, D], BF16)
-            nc.scalar.activation(out=junk_w[:], in_=pw[:], func=ACT.Square, accum_out=sums[:, 0:1])
-            nc.scalar.activation(out=junk_w[:], in_=aw[:], func=ACT.Square, accum_out=sums[:, 1:2])
+        def setup_sums():
+            for s0, s1, i in ((pw, pw, 0), (aw, aw, 1), (pw, aw, 2)):
+                junk_w = work.tile([P, D], BF16, name="junk_v")
+                nc.vector.scalar_tensor_tensor(out=junk_w[:], in0=s0[:], scalar=1.0, in1=s1[:], op0=ALU.mult, op1=ALU.mult, accum_out=sums[:, i:i + 1])
             nc.scalar.activation(out=ran[:], in_=sums[:, 1:2], func=ACT.Abs_reciprocal_sqrt)
 
         def setup_rest():
@@ -227,9 +241,6 @@ def tile_hyperbolicmlr_t_kernel(tc, x, a, p, out):
                     nc.tensor.transpose(pwt[:, i, w, :], words[:, w * P:(w + 1) * P], ident[:])
             gw = const.tile([P, 2 * P * 4], BF16, align_bytes=64)
             nc.vector.tensor_copy(out=gw[:].bitcast(F32).rearrange("k (i c w) -> k i c w", i=2, w=KW), in_=pwt[:].rearrange("k i w c -> k i c w"))
-            junk_p = const.tile([P, D], BF16)
-            pa = const.tile([P, 1], F32)
-            nc.vector.scalar_tensor_tensor(out=junk_p[:], in0=pw[:], scalar=1.0, in1=aw[:], op0=ALU.mult, op1=ALU.mult, accum_out=pa[:])
             nc.vector.quantize_mx(out=w_codes[:].bitcast(FP8X4), scales=w_scales[:], in_=gw[:])
             nc.vector.tensor_scalar(out=beta[:], in0=sums[:, 0:1], scalar1=-1.0, scalar2=1.0, op0=ALU.mult, op1=ALU.add)
             safe = const.tile([P, 1], F32)
@@ -238,14 +249,17 @@ def tile_hyperbolicmlr_t_kernel(tc, x, a, p, out):
             rb = const.tile([P, 1], F32)
             nc.vector.reciprocal(out=rb[:], in_=safe[:])
             nc.vector.tensor_scalar(out=nhb[:], in0=beta[:], scalar1=-0.5, scalar2=None, op0=ALU.mult)
-            nc.vector.tensor_scalar(out=fcol[:], in0=pa[:], scalar1=rb[:], scalar2=-1.0, op0=ALU.mult, op1=ALU.mult)
+            nc.vector.tensor_scalar(out=fcol[:], in0=sums[:, 2:3], scalar1=rb[:], scalar2=-1.0, op0=ALU.mult, op1=ALU.mult)
             nc.vector.tensor_scalar(out=ecol[:], in0=safe[:], scalar1=ran[:], scalar2=-1.0, op0=ALU.mult, op1=ALU.mult)
 
-        for k in range(-5, NCH + 4):
+        nturn = 0
+        for k in range(-5, NCH + 3):
             if ok(k + 5 + PRE):
                 load(k + 5 + PRE)
             first = halves(k + 3)[0] if ok(k + 3) else None
             second = halves(k + 3)[1] if ok(k + 3) and len(halves(k + 3)) > 1 else None
+            if ok(k + 5):
+                norms_v(k + 5)
             if ok(k + 1):
                 quant(k + 1)
                 mx(k + 1)
@@ -276,31 +290,27 @@ def tile_hyperbolicmlr_t_kernel(tc, x, a, p, out):
                 transp(k + 3, *second)
             if ok(k):
                 form_t(k)
+            if k == -4:
+                setup_sums()
             if k == -3:
                 setup_rest()
             if ok(k - 2):
                 square_z(k - 2)
             if ok(k + 5):
-                norms_v(k + 5)
                 norms_s(k + 5)
             if ok(k - 2):
                 inv_h(k - 2)
-            if k == -5:
-                setup_scalar()
             if ok(k - 1):
                 form_z(k - 1)
-            if ok(k - 3):
-                form_h(k - 3)
+            if k >= NCH - 1:
+                for i in range(2):
+                    turn(nturn)
+                    nturn += 1
 
-        banks = ((ps_t, "pt"), (ps_u, "pu"), (ps_v, "pv"), (ps_t, "pt"), (ps_u, "pu"), (ps_v, "pv"), (ps_t, "pt"), (ps_s, "pb"))
-        for c in range(NCH):
+        for i, c in enumerate(order):
             n = SIZES[c]
-            pool, nm = banks[c % len(banks)]
-            acc = pool.tile([P, n, P], F32, name=nm)
-            for j in range(n):
-                cols = slice(j * P, (j + 1) * P)
-                nc.tensor.matmul(acc[:, j, :], lhsT=T["tm", c][:, cols], rhs=ident[:], start=True, stop=False, is_transpose=True)
-                nc.tensor.matmul(acc[:, j, :], lhsT=T["sq", c][:, cols], rhs=ident[:], start=False, stop=True, is_transpose=True)
+            if i >= nturn:
+                turn(i)
             res = stage.tile([P, n, P], F32, name="res")
-            nc.scalar.activation(out=res[:], in_=acc[:], func=ACT.Ln)
+            nc.scalar.activation(out=res[:], in_=T["acc", c][:], func=ACT.Ln)
             nc.sync.dma_start(out=ov[:, STARTS[c]:STARTS[c] + n, :], in_=res[:])

@@ -41,6 +41,7 @@ def tile_hyperbolicmlr_t_kernel(tc, x, a, p, out):
         small = ctx.enter_context(tc.tile_pool(name="small", bufs=9))
         work = ctx.enter_context(tc.tile_pool(name="work", bufs=2))
         work3 = ctx.enter_context(tc.tile_pool(name="work3", bufs=3))
+        work4 = ctx.enter_context(tc.tile_pool(name="work4", bufs=4))
         stage = ctx.enter_context(tc.tile_pool(name="stage", bufs=8))
         ps_t = ctx.enter_context(tc.psum_pool(name="ps_t", bufs=3))
         ps_u = ctx.enter_context(tc.psum_pool(name="ps_u", bufs=2))
@@ -141,7 +142,7 @@ def tile_hyperbolicmlr_t_kernel(tc, x, a, p, out):
             T["pb", c] = pb
 
         def copy_s1(c):
-            sb = work3.tile([P, SIZES[c] * P], F32, name="sb")
+            sb = work4.tile([P, SIZES[c] * P], F32, name="sb")
             nc.scalar.copy(out=sb[:], in_=T["pb", c][:].rearrange("k j r -> k (j r)"))
             T["sb", c] = sb
 
@@ -260,10 +261,11 @@ def tile_hyperbolicmlr_t_kernel(tc, x, a, p, out):
             second = halves(k + 3)[1] if ok(k + 3) and len(halves(k + 3)) > 1 else None
             if ok(k + 5):
                 norms_v(k + 5)
+            if ok(k + 2):
+                spread(k + 2)
             if ok(k + 1):
                 quant(k + 1)
                 mx(k + 1)
-                spread(k + 1)
             if ok(k - 1):
                 square_t(k - 1)
             if ok(k + 2):
@@ -275,8 +277,8 @@ def tile_hyperbolicmlr_t_kernel(tc, x, a, p, out):
             if ok(k + 4):
                 inv_norm(k + 4)
                 factor(k + 4)
-            if ok(k + 1):
-                copy_s1(k + 1)
+            if ok(k + 2):
+                copy_s1(k + 2)
             if ok(k):
                 form_a(k)
             if first:

@@ -22,11 +22,20 @@ SIZES = (1, 1, 2) + (4,) * 14 + (2, 2)
 NCH = len(SIZES)
 STARTS = tuple(sum(SIZES[:i]) for i in range(NCH))
 PRE = 5
+FAR = 16
+TURNS = {-3: 1, -2: 1, -1: 2, 0: 2, 1: 2}
 
 
 def norms_on_vector(c):
-    n = SIZES[c]
-    return n // 2
+    return 1 if 3 < c < 8 else 0
+
+
+def norms_iteration(c):
+    return c - (5 if c < 7 else 6 if c < 10 else 7 if c < 13 else 8)
+
+
+def evac_on_vector(c, h):
+    return c > 2 and (c < 13 or h == 0)
 
 
 def tile_hyperbolicmlr_t_kernel(tc, x, a, p, out):
@@ -37,8 +46,8 @@ def tile_hyperbolicmlr_t_kernel(tc, x, a, p, out):
     with ExitStack() as ctx:
         const = ctx.enter_context(tc.tile_pool(name="const", bufs=1))
         keep = ctx.enter_context(tc.tile_pool(name="keep", bufs=1))
-        xin = ctx.enter_context(tc.tile_pool(name="xin", bufs=8))
-        small = ctx.enter_context(tc.tile_pool(name="small", bufs=9))
+        xin = ctx.enter_context(tc.tile_pool(name="xin", bufs=9))
+        small = ctx.enter_context(tc.tile_pool(name="small", bufs=12))
         work = ctx.enter_context(tc.tile_pool(name="work", bufs=2))
         work3 = ctx.enter_context(tc.tile_pool(name="work3", bufs=3))
         work4 = ctx.enter_context(tc.tile_pool(name="work4", bufs=4))
@@ -68,8 +77,10 @@ def tile_hyperbolicmlr_t_kernel(tc, x, a, p, out):
                 junk = work.tile([P, D], BF16, name="junk_v")
                 nc.vector.scalar_tensor_tensor(out=junk[:], in0=xj, scalar=1.0, in1=xj, op0=ALU.mult, op1=ALU.mult, accum_out=T["n2", c][:, j:j + 1])
 
-        def norms_s(c):
-            for j in range(norms_on_vector(c), SIZES[c]):
+        def norms_s(c, part, parts):
+            first = norms_on_vector(c)
+            tiles = range(first, SIZES[c])
+            for j in tiles[part * len(tiles) // parts:(part + 1) * len(tiles) // parts]:
                 junk = work.tile([P, D], BF16, name="junk_s")
                 nc.scalar.activation(out=junk[:], in_=T["xr", c][:, j, :], func=ACT.Square, accum_out=T["n2", c][:, j:j + 1])
 
@@ -78,14 +89,20 @@ def tile_hyperbolicmlr_t_kernel(tc, x, a, p, out):
             nc.scalar.activation(out=rn[:], in_=T["n2", c][:], func=ACT.Abs_reciprocal_sqrt)
             T["rn", c] = rn
 
-        def factor(c):
+        def plus_one(c):
             n = SIZES[c]
-            sc = small.tile([P, n], F32, name="sc")
-            nc.gpsimd.tensor_scalar(out=sc[:], in0=T["rn", c][:], scalar1=MAXN, scalar2=1.0, op0=ALU.mult, op1=ALU.min)
-            s1 = small.tile([P, n], F32, name="s1")
-            nc.gpsimd.tensor_scalar(out=s1[:], in0=T["n2", c][:], scalar1=MAXN * MAXN, scalar2=1.0, op0=ALU.min, op1=ALU.add)
-            T["sc", c] = sc
+            if STARTS[c] < FAR:
+                near = small.tile([P, n], F32, name="s1")
+                s1 = near[:]
+            else:
+                s1 = far_in[STARTS[c] // FAR][:, STARTS[c] % FAR:STARTS[c] % FAR + n]
+            nc.gpsimd.tensor_scalar(out=s1, in0=T["n2", c][:], scalar1=MAXN * MAXN, scalar2=1.0, op0=ALU.min, op1=ALU.add)
             T["s1", c] = s1
+
+        def factor(c):
+            sc = small.tile([P, SIZES[c]], F32, name="sc")
+            nc.gpsimd.tensor_scalar(out=sc[:], in0=T["rn", c][:], scalar1=MAXN, scalar2=1.0, op0=ALU.mult, op1=ALU.min)
+            T["sc", c] = sc
 
         def halves(c):
             n = SIZES[c]
@@ -109,7 +126,11 @@ def tile_hyperbolicmlr_t_kernel(tc, x, a, p, out):
             if h == 0:
                 T["gx", c] = work3.tile([P, SIZES[c] * P * 4], BF16, name="gx", align_bytes=64)
             dst = T["gx", c][:].bitcast(F32).rearrange("k (j r w) -> k j r w", r=P, w=KW)[:, 2 * h:2 * h + m, :, :]
-            nc.scalar.copy(out=dst, in_=T["pt", c, h][:].rearrange("k j w r -> k j r w"))
+            src = T["pt", c, h][:].rearrange("k j w r -> k j r w")
+            if evac_on_vector(c, h):
+                nc.vector.tensor_copy(out=dst, in_=src)
+            else:
+                nc.scalar.copy(out=dst, in_=src)
 
         def quant(c):
             n = SIZES[c]
@@ -144,16 +165,34 @@ def tile_hyperbolicmlr_t_kernel(tc, x, a, p, out):
         def copy_s1(c):
             sb = work4.tile([P, SIZES[c] * P], F32, name="sb")
             nc.scalar.copy(out=sb[:], in_=T["pb", c][:].rearrange("k j r -> k (j r)"))
-            T["sb", c] = sb
+            T["sb", c] = sb[:]
+
+        def turn_far(g):
+            pb = ps_s.tile([P, P], F32, name="pb")
+            nc.tensor.transpose(pb[:], far_in[g][:], ident[:])
+            T["far", g] = pb
+
+        def send_far(g):
+            pb = T["far", g]
+            rows = work.tile([P, P], F32, name="rows")
+            nc.scalar.copy(out=rows[:], in_=pb[:])
+            rest = out[g * FAR:(g + 1) * FAR, :]
+            nc.sync.dma_start(out=rest, in_=rows[0:FAR, :])
+            sb = keep.tile([P, FAR * P], F32, name="far%d" % g)
+            nc.sync.dma_start(out=sb[:], in_=rest.rearrange("j r -> (j r)").partition_broadcast(P))
+            for c in range(NCH):
+                if STARTS[c] // FAR == g:
+                    o = STARTS[c] % FAR
+                    T["sb", c] = sb[:, o * P:(o + SIZES[c]) * P]
 
         def form_a(c):
             ta = work.tile([P, SIZES[c] * P], F32, name="ta")
-            nc.vector.scalar_tensor_tensor(out=ta[:], in0=T["pu", c][:], scalar=-2.0, in1=T["sb", c][:], op0=ALU.mult, op1=ALU.add)
+            nc.vector.scalar_tensor_tensor(out=ta[:], in0=T["pu", c][:], scalar=-2.0, in1=T["sb", c], op0=ALU.mult, op1=ALU.add)
             T["ta", c] = ta
 
         def form_r(c):
             tt = work3.tile([P, SIZES[c] * P], F32, name="tt")
-            nc.vector.tensor_scalar(out=tt[:], in0=T["ta", c][:], scalar1=beta[:], scalar2=None, op0=ALU.max)
+            nc.gpsimd.tensor_scalar(out=tt[:], in0=T["ta", c][:], scalar1=3e38, scalar2=beta[:], op0=ALU.min, op1=ALU.max)
             T["tt", c] = tt
 
         def form_m(c):
@@ -163,7 +202,7 @@ def tile_hyperbolicmlr_t_kernel(tc, x, a, p, out):
 
         def form_t(c):
             tt = T["tt", c]
-            nc.vector.scalar_tensor_tensor(out=tt[:], in0=T["sb", c][:], scalar=nhb[:], in1=tt[:], op0=ALU.mult, op1=ALU.add)
+            nc.vector.scalar_tensor_tensor(out=tt[:], in0=T["sb", c], scalar=nhb[:], in1=tt[:], op0=ALU.mult, op1=ALU.add)
 
         def square_t(c):
             tt = T["tt", c]
@@ -192,7 +231,7 @@ def tile_hyperbolicmlr_t_kernel(tc, x, a, p, out):
             nc.vector.scalar_tensor_tensor(out=sq[:], in0=sq[:], scalar=1.0, in1=T["tg", c][:], op0=ALU.add, op1=ALU.mult)
 
         order = list(range(3, NCH)) + [2, 1, 0]
-        banks = ((ps_t, "pt"), (ps_t, "pt"), (ps_t, "pt"), (ps_s, "pb"), (ps_u, "pu"), (ps_v, "pv"), (ps_u, "pu"), (ps_v, "pv"))
+        banks = ((ps_s, "pb"), (ps_t, "pt"), (ps_t, "pt"), (ps_t, "pt"), (ps_u, "pu"), (ps_v, "pv"), (ps_u, "pu"), (ps_v, "pv"))
 
         def turn(i):
             c = order[i]
@@ -223,6 +262,10 @@ def tile_hyperbolicmlr_t_kernel(tc, x, a, p, out):
         nhb = const.tile([P, 1], F32)
         fcol = const.tile([P, 1], F32)
         ecol = const.tile([P, 1], F32)
+        far_in = {}
+        for g in range(1, NT // FAR):
+            far_in[g] = const.tile([P, P], F32, name="far_in%d" % g)
+            nc.gpsimd.memset(far_in[g][:], 0.0)
         sums = const.tile([P, 3], F32)
         ran = const.tile([P, 1], F32)
         w_codes = const.tile([P, 2 * P], U32, align_bytes=64)
@@ -259,34 +302,50 @@ def tile_hyperbolicmlr_t_kernel(tc, x, a, p, out):
                 load(k + 5 + PRE)
             first = halves(k + 3)[0] if ok(k + 3) else None
             second = halves(k + 3)[1] if ok(k + 3) and len(halves(k + 3)) > 1 else None
-            if ok(k + 5):
-                norms_v(k + 5)
-            if ok(k + 2):
+            fresh = [c for c in range(NCH) if norms_iteration(c) == k]
+            for c in fresh:
+                norms_v(c)
+                if k <= 0:
+                    norms_s(c, 0, 1)
+            groups = []
+            for c in range(NCH):
+                if norms_iteration(c) == k - 1:
+                    plus_one(c)
+                    if STARTS[c] >= FAR and (STARTS[c] + SIZES[c]) % FAR == 0:
+                        groups.append(STARTS[c] // FAR)
+            for g in groups:
+                turn_far(g)
+            if ok(k + 2) and STARTS[k + 2] < FAR:
                 spread(k + 2)
             if ok(k + 1):
                 quant(k + 1)
                 mx(k + 1)
             if ok(k - 1):
                 square_t(k - 1)
+            if ok(k):
+                form_a(k)
+                form_r(k)
             if ok(k + 2):
                 evac(k + 2, *halves(k + 2)[0])
-            if ok(k - 1):
-                inv_t(k - 1)
+            if ok(k):
+                form_m(k)
             if ok(k + 2) and len(halves(k + 2)) > 1:
                 evac(k + 2, *halves(k + 2)[1])
+            for c in fresh:
+                if k > 0:
+                    norms_s(c, 0, 2)
+            if ok(k - 1):
+                inv_t(k - 1)
             if ok(k + 4):
                 inv_norm(k + 4)
                 factor(k + 4)
-            if ok(k + 2):
-                copy_s1(k + 2)
-            if ok(k):
-                form_a(k)
             if first:
                 scale(k + 3, *first)
                 transp(k + 3, *first)
-            if ok(k):
-                form_r(k)
-                form_m(k)
+            for g in groups:
+                send_far(g)
+            if ok(k + 2) and STARTS[k + 2] < FAR:
+                copy_s1(k + 2)
             if second:
                 scale(k + 3, *second)
                 transp(k + 3, *second)
@@ -298,16 +357,16 @@ def tile_hyperbolicmlr_t_kernel(tc, x, a, p, out):
                 setup_rest()
             if ok(k - 2):
                 square_z(k - 2)
-            if ok(k + 5):
-                norms_s(k + 5)
+            for c in fresh:
+                if k > 0:
+                    norms_s(c, 1, 2)
             if ok(k - 2):
                 inv_h(k - 2)
             if ok(k - 1):
                 form_z(k - 1)
-            if k >= NCH - 1:
-                for i in range(2):
-                    turn(nturn)
-                    nturn += 1
+            for i in range(TURNS.get(k - NCH, 0)):
+                turn(nturn)
+                nturn += 1
 
         for i, c in enumerate(order):
             n = SIZES[c]

@@ -27,15 +27,15 @@ TURNS = {-3: 1, -2: 1, -1: 2, 0: 2, 1: 2}
 
 
 def norms_on_vector(c):
-    return 1 if 3 < c < 8 else 0
+    return 0 if SIZES[c] < 4 else 2 if c < 6 else 1 if c % 2 == 0 else 0
 
 
 def norms_iteration(c):
-    return c - (5 if c < 7 else 6 if c < 10 else 7 if c < 13 else 8)
+    return c - (5 if c < 6 else 6 if c < 9 else 7 if c < 13 else 8)
 
 
 def evac_on_vector(c, h):
-    return c > 2 and (c < 13 or h == 0)
+    return c >= 0
 
 
 def tile_hyperbolicmlr_t_kernel(tc, x, a, p, out):
@@ -197,7 +197,7 @@ def tile_hyperbolicmlr_t_kernel(tc, x, a, p, out):
 
         def form_m(c):
             tm = keep.tile([P, SIZES[c] * P], F32, name="tm%d" % c)
-            nc.vector.scalar_tensor_tensor(out=tm[:], in0=T["ta", c][:], scalar=fcol[:], in1=T["pv", c][:], op0=ALU.mult, op1=ALU.add)
+            nc.vector.scalar_tensor_tensor(out=tm[:], in0=T["ta", c][:], scalar=fcol[:], in1=T["pv", c][:], op0=ALU.mult, op1=ALU.subtract)
             T["tm", c] = tm
 
         def form_t(c):
@@ -206,7 +206,7 @@ def tile_hyperbolicmlr_t_kernel(tc, x, a, p, out):
 
         def square_t(c):
             tt = T["tt", c]
-            nc.scalar.activation(out=tt[:], in_=tt[:], func=ACT.Square)
+            nc.scalar.activation(out=tt[:], in_=tt[:], func=ACT.Square, scale=tcol[:])
 
         def inv_t(c):
             tt = T["tt", c]
@@ -214,7 +214,8 @@ def tile_hyperbolicmlr_t_kernel(tc, x, a, p, out):
 
         def form_z(c):
             tm = T["tm", c]
-            nc.vector.scalar_tensor_tensor(out=tm[:], in0=tm[:], scalar=ecol[:], in1=T["tt", c][:], op0=ALU.mult, op1=ALU.mult)
+            engine = nc.gpsimd if c < NCH - 2 else nc.vector
+            engine.tensor_tensor(out=tm[:], in0=tm[:], in1=T["tt", c][:], op=ALU.mult)
 
         def square_z(c):
             sq = keep.tile([P, SIZES[c] * P], F32, name="sq%d" % c)
@@ -261,11 +262,14 @@ def tile_hyperbolicmlr_t_kernel(tc, x, a, p, out):
         beta = const.tile([P, 1], F32)
         nhb = const.tile([P, 1], F32)
         fcol = const.tile([P, 1], F32)
-        ecol = const.tile([P, 1], F32)
+        tcol = const.tile([P, 1], F32)
         far_in = {}
         for g in range(1, NT // FAR):
             far_in[g] = const.tile([P, P], F32, name="far_in%d" % g)
             nc.gpsimd.memset(far_in[g][:], 0.0)
+        asw = const.tile([P, D], BF16)
+        sgn = const.tile([P, 1], F32)
+        gw = const.tile([P, 2 * P * 4], BF16, align_bytes=64)
         sums = const.tile([P, 3], F32)
         ran = const.tile([P, 1], F32)
         w_codes = const.tile([P, 2 * P], U32, align_bytes=64)
@@ -277,24 +281,29 @@ def tile_hyperbolicmlr_t_kernel(tc, x, a, p, out):
                 nc.vector.scalar_tensor_tensor(out=junk_w[:], in0=s0[:], scalar=1.0, in1=s1[:], op0=ALU.mult, op1=ALU.mult, accum_out=sums[:, i:i + 1])
             nc.scalar.activation(out=ran[:], in_=sums[:, 1:2], func=ACT.Abs_reciprocal_sqrt)
 
-        def setup_rest():
+        def setup_signs():
+            nc.vector.tensor_scalar(out=beta[:], in0=sums[:, 0:1], scalar1=-1.0, scalar2=1.0, op0=ALU.mult, op1=ALU.add)
+            nc.vector.tensor_scalar(out=sgn[:], in0=beta[:], scalar1=0.0, scalar2=2.0, op0=ALU.is_ge, op1=ALU.mult)
+            nc.vector.tensor_scalar(out=sgn[:], in0=sgn[:], scalar1=-1.0, scalar2=None, op0=ALU.add)
+            nc.vector.tensor_scalar(out=asw[:], in0=aw[:], scalar1=sgn[:], scalar2=None, op0=ALU.mult)
+
+        def setup_turn():
             pwt = ps_t.tile([P, 2, KW, P], F32, name="pt")
-            for i, src in enumerate((pw, aw)):
+            for i, src in enumerate((pw, asw)):
                 words = src[:].bitcast(F32)
                 for w in range(KW):
                     nc.tensor.transpose(pwt[:, i, w, :], words[:, w * P:(w + 1) * P], ident[:])
-            gw = const.tile([P, 2 * P * 4], BF16, align_bytes=64)
-            nc.vector.tensor_copy(out=gw[:].bitcast(F32).rearrange("k (i c w) -> k i c w", i=2, w=KW), in_=pwt[:].rearrange("k i w c -> k i c w"))
-            nc.vector.quantize_mx(out=w_codes[:].bitcast(FP8X4), scales=w_scales[:], in_=gw[:])
-            nc.vector.tensor_scalar(out=beta[:], in0=sums[:, 0:1], scalar1=-1.0, scalar2=1.0, op0=ALU.mult, op1=ALU.add)
-            safe = const.tile([P, 1], F32)
-            nc.vector.tensor_scalar(out=safe[:], in0=beta[:], scalar1=0.0, scalar2=1e-20, op0=ALU.is_equal, op1=ALU.mult)
-            nc.vector.tensor_tensor(out=safe[:], in0=safe[:], in1=beta[:], op=ALU.add)
+            nc.scalar.copy(out=gw[:].bitcast(F32).rearrange("k (i c w) -> k i c w", i=2, w=KW), in_=pwt[:].rearrange("k i w c -> k i c w"))
+
+        def setup_rest():
+            absb = const.tile([P, 1], F32)
+            nc.vector.tensor_scalar(out=absb[:], in0=beta[:], scalar1=sgn[:], scalar2=1e-9, op0=ALU.mult, op1=ALU.max)
             rb = const.tile([P, 1], F32)
-            nc.vector.reciprocal(out=rb[:], in_=safe[:])
+            nc.vector.reciprocal(out=rb[:], in_=absb[:])
             nc.vector.tensor_scalar(out=nhb[:], in0=beta[:], scalar1=-0.5, scalar2=None, op0=ALU.mult)
-            nc.vector.tensor_scalar(out=fcol[:], in0=sums[:, 2:3], scalar1=rb[:], scalar2=-1.0, op0=ALU.mult, op1=ALU.mult)
-            nc.vector.tensor_scalar(out=ecol[:], in0=safe[:], scalar1=ran[:], scalar2=-1.0, op0=ALU.mult, op1=ALU.mult)
+            nc.vector.tensor_scalar(out=fcol[:], in0=sums[:, 2:3], scalar1=rb[:], scalar2=None, op0=ALU.mult)
+            nc.vector.tensor_scalar(out=tcol[:], in0=rb[:], scalar1=ran[:], scalar2=sums[:, 1:2], op0=ALU.mult, op1=ALU.mult)
+            nc.vector.quantize_mx(out=w_codes[:].bitcast(FP8X4), scales=w_scales[:], in_=gw[:])
 
         nturn = 0
         for k in range(-5, NCH + 3):
@@ -303,6 +312,9 @@ def tile_hyperbolicmlr_t_kernel(tc, x, a, p, out):
             first = halves(k + 3)[0] if ok(k + 3) else None
             second = halves(k + 3)[1] if ok(k + 3) and len(halves(k + 3)) > 1 else None
             fresh = [c for c in range(NCH) if norms_iteration(c) == k]
+            if ok(k + 4) and k <= 0:
+                inv_norm(k + 4)
+                factor(k + 4)
             for c in fresh:
                 norms_v(c)
                 if k <= 0:
@@ -313,8 +325,6 @@ def tile_hyperbolicmlr_t_kernel(tc, x, a, p, out):
                     plus_one(c)
                     if STARTS[c] >= FAR and (STARTS[c] + SIZES[c]) % FAR == 0:
                         groups.append(STARTS[c] // FAR)
-            for g in groups:
-                turn_far(g)
             if ok(k + 2) and STARTS[k + 2] < FAR:
                 spread(k + 2)
             if ok(k + 1):
@@ -333,37 +343,47 @@ def tile_hyperbolicmlr_t_kernel(tc, x, a, p, out):
                 evac(k + 2, *halves(k + 2)[1])
             for c in fresh:
                 if k > 0:
-                    norms_s(c, 0, 2)
+                    norms_s(c, 0, 4)
             if ok(k - 1):
                 inv_t(k - 1)
-            if ok(k + 4):
+                form_z(k - 1)
+            for c in fresh:
+                if k > 0:
+                    norms_s(c, 1, 4)
+            if ok(k + 4) and k > 0:
                 inv_norm(k + 4)
                 factor(k + 4)
             if first:
                 scale(k + 3, *first)
                 transp(k + 3, *first)
-            for g in groups:
-                send_far(g)
             if ok(k + 2) and STARTS[k + 2] < FAR:
                 copy_s1(k + 2)
             if second:
                 scale(k + 3, *second)
                 transp(k + 3, *second)
+            for g in groups:
+                turn_far(g)
             if ok(k):
                 form_t(k)
             if k == -4:
                 setup_sums()
             if k == -3:
+                setup_signs()
+                setup_turn()
+            if k == -2:
                 setup_rest()
             if ok(k - 2):
                 square_z(k - 2)
             for c in fresh:
                 if k > 0:
-                    norms_s(c, 1, 2)
+                    norms_s(c, 2, 4)
             if ok(k - 2):
                 inv_h(k - 2)
-            if ok(k - 1):
-                form_z(k - 1)
+            for c in fresh:
+                if k > 0:
+                    norms_s(c, 3, 4)
+            for g in groups:
+                send_far(g)
             for i in range(TURNS.get(k - NCH, 0)):
                 turn(nturn)
                 nturn += 1

@@ -27,7 +27,7 @@ TURNS = {-3: 1, -2: 1, -1: 2, 0: 2, 1: 2}
 
 
 def norms_on_vector(c):
-    return 0 if SIZES[c] < 4 else 2 if c < 6 else 1 if c % 2 == 0 else 0
+    return 0 if SIZES[c] < 4 else 2 if c < 6 else 0
 
 
 def norms_iteration(c):
@@ -35,7 +35,7 @@ def norms_iteration(c):
 
 
 def evac_on_vector(c, h):
-    return c >= 0
+    return c < 13 or h == 0
 
 
 def tile_hyperbolicmlr_t_kernel(tc, x, a, p, out):
@@ -197,7 +197,7 @@ def tile_hyperbolicmlr_t_kernel(tc, x, a, p, out):
 
         def form_m(c):
             tm = keep.tile([P, SIZES[c] * P], F32, name="tm%d" % c)
-            nc.vector.scalar_tensor_tensor(out=tm[:], in0=T["ta", c][:], scalar=fcol[:], in1=T["pv", c][:], op0=ALU.mult, op1=ALU.subtract)
+            nc.vector.scalar_tensor_tensor(out=tm[:], in0=T["ta", c][:], scalar=fcol[:], in1=T["pv", c][:], op0=ALU.mult, op1=ALU.add)
             T["tm", c] = tm
 
         def form_t(c):
@@ -206,7 +206,7 @@ def tile_hyperbolicmlr_t_kernel(tc, x, a, p, out):
 
         def square_t(c):
             tt = T["tt", c]
-            nc.scalar.activation(out=tt[:], in_=tt[:], func=ACT.Square, scale=tcol[:])
+            nc.scalar.activation(out=tt[:], in_=tt[:], func=ACT.Square)
 
         def inv_t(c):
             tt = T["tt", c]
@@ -214,8 +214,7 @@ def tile_hyperbolicmlr_t_kernel(tc, x, a, p, out):
 
         def form_z(c):
             tm = T["tm", c]
-            engine = nc.gpsimd if c < NCH - 2 else nc.vector
-            engine.tensor_tensor(out=tm[:], in0=tm[:], in1=T["tt", c][:], op=ALU.mult)
+            nc.vector.scalar_tensor_tensor(out=tm[:], in0=tm[:], scalar=ecol[:], in1=T["tt", c][:], op0=ALU.mult, op1=ALU.mult)
 
         def square_z(c):
             sq = keep.tile([P, SIZES[c] * P], F32, name="sq%d" % c)
@@ -239,8 +238,14 @@ def tile_hyperbolicmlr_t_kernel(tc, x, a, p, out):
             pool, nm = banks[i % len(banks)]
             form_h(c)
             acc = pool.tile([P, SIZES[c], P], F32, name=nm)
+            on_vector = i >= len(banks) and i % 2 == 1
+            if on_vector:
+                nc.vector.tensor_tensor(out=T["sq", c][:], in0=T["sq", c][:], in1=T["tm", c][:], op=ALU.add)
             for j in range(SIZES[c]):
                 cols = slice(j * P, (j + 1) * P)
+                if on_vector:
+                    nc.tensor.transpose(acc[:, j, :], T["sq", c][:, cols], ident[:])
+                    continue
                 nc.tensor.matmul(acc[:, j, :], lhsT=T["tm", c][:, cols], rhs=ident[:], start=True, stop=False, is_transpose=True)
                 nc.tensor.matmul(acc[:, j, :], lhsT=T["sq", c][:, cols], rhs=ident[:], start=False, stop=True, is_transpose=True)
             T["acc", c] = acc
@@ -262,13 +267,11 @@ def tile_hyperbolicmlr_t_kernel(tc, x, a, p, out):
         beta = const.tile([P, 1], F32)
         nhb = const.tile([P, 1], F32)
         fcol = const.tile([P, 1], F32)
-        tcol = const.tile([P, 1], F32)
+        ecol = const.tile([P, 1], F32)
         far_in = {}
         for g in range(1, NT // FAR):
             far_in[g] = const.tile([P, P], F32, name="far_in%d" % g)
             nc.gpsimd.memset(far_in[g][:], 0.0)
-        asw = const.tile([P, D], BF16)
-        sgn = const.tile([P, 1], F32)
         gw = const.tile([P, 2 * P * 4], BF16, align_bytes=64)
         sums = const.tile([P, 3], F32)
         ran = const.tile([P, 1], F32)
@@ -281,28 +284,24 @@ def tile_hyperbolicmlr_t_kernel(tc, x, a, p, out):
                 nc.vector.scalar_tensor_tensor(out=junk_w[:], in0=s0[:], scalar=1.0, in1=s1[:], op0=ALU.mult, op1=ALU.mult, accum_out=sums[:, i:i + 1])
             nc.scalar.activation(out=ran[:], in_=sums[:, 1:2], func=ACT.Abs_reciprocal_sqrt)
 
-        def setup_signs():
-            nc.vector.tensor_scalar(out=beta[:], in0=sums[:, 0:1], scalar1=-1.0, scalar2=1.0, op0=ALU.mult, op1=ALU.add)
-            nc.vector.tensor_scalar(out=sgn[:], in0=beta[:], scalar1=0.0, scalar2=2.0, op0=ALU.is_ge, op1=ALU.mult)
-            nc.vector.tensor_scalar(out=sgn[:], in0=sgn[:], scalar1=-1.0, scalar2=None, op0=ALU.add)
-            nc.vector.tensor_scalar(out=asw[:], in0=aw[:], scalar1=sgn[:], scalar2=None, op0=ALU.mult)
-
         def setup_turn():
             pwt = ps_t.tile([P, 2, KW, P], F32, name="pt")
-            for i, src in enumerate((pw, asw)):
+            for i, src in enumerate((pw, aw)):
                 words = src[:].bitcast(F32)
                 for w in range(KW):
                     nc.tensor.transpose(pwt[:, i, w, :], words[:, w * P:(w + 1) * P], ident[:])
             nc.scalar.copy(out=gw[:].bitcast(F32).rearrange("k (i c w) -> k i c w", i=2, w=KW), in_=pwt[:].rearrange("k i w c -> k i c w"))
 
         def setup_rest():
-            absb = const.tile([P, 1], F32)
-            nc.vector.tensor_scalar(out=absb[:], in0=beta[:], scalar1=sgn[:], scalar2=1e-9, op0=ALU.mult, op1=ALU.max)
+            nc.vector.tensor_scalar(out=beta[:], in0=sums[:, 0:1], scalar1=-1.0, scalar2=1.0, op0=ALU.mult, op1=ALU.add)
+            safe = const.tile([P, 1], F32)
+            nc.vector.tensor_scalar(out=safe[:], in0=beta[:], scalar1=0.0, scalar2=1e-20, op0=ALU.is_equal, op1=ALU.mult)
+            nc.vector.tensor_tensor(out=safe[:], in0=safe[:], in1=beta[:], op=ALU.add)
             rb = const.tile([P, 1], F32)
-            nc.vector.reciprocal(out=rb[:], in_=absb[:])
+            nc.vector.reciprocal(out=rb[:], in_=safe[:])
             nc.vector.tensor_scalar(out=nhb[:], in0=beta[:], scalar1=-0.5, scalar2=None, op0=ALU.mult)
-            nc.vector.tensor_scalar(out=fcol[:], in0=sums[:, 2:3], scalar1=rb[:], scalar2=None, op0=ALU.mult)
-            nc.vector.tensor_scalar(out=tcol[:], in0=rb[:], scalar1=ran[:], scalar2=sums[:, 1:2], op0=ALU.mult, op1=ALU.mult)
+            nc.vector.tensor_scalar(out=fcol[:], in0=sums[:, 2:3], scalar1=rb[:], scalar2=-1.0, op0=ALU.mult, op1=ALU.mult)
+            nc.vector.tensor_scalar(out=ecol[:], in0=safe[:], scalar1=ran[:], scalar2=-1.0, op0=ALU.mult, op1=ALU.mult)
             nc.vector.quantize_mx(out=w_codes[:].bitcast(FP8X4), scales=w_scales[:], in_=gw[:])
 
         nturn = 0
@@ -346,7 +345,6 @@ def tile_hyperbolicmlr_t_kernel(tc, x, a, p, out):
                     norms_s(c, 0, 4)
             if ok(k - 1):
                 inv_t(k - 1)
-                form_z(k - 1)
             for c in fresh:
                 if k > 0:
                     norms_s(c, 1, 4)
@@ -368,7 +366,6 @@ def tile_hyperbolicmlr_t_kernel(tc, x, a, p, out):
             if k == -4:
                 setup_sums()
             if k == -3:
-                setup_signs()
                 setup_turn()
             if k == -2:
                 setup_rest()
@@ -384,6 +381,8 @@ def tile_hyperbolicmlr_t_kernel(tc, x, a, p, out):
                     norms_s(c, 3, 4)
             for g in groups:
                 send_far(g)
+            if ok(k - 1):
+                form_z(k - 1)
             for i in range(TURNS.get(k - NCH, 0)):
                 turn(nturn)
                 nturn += 1

@@ -27,7 +27,7 @@ TURNS = {-3: 1, -2: 1, -1: 2, 0: 2, 1: 2}
 
 
 def norms_on_vector(c):
-    return 0 if SIZES[c] < 4 else 2 if c < 6 else 0
+    return 0 if SIZES[c] < 4 else 2 if c < 6 else 1 if c % 2 == 0 else 0
 
 
 def norms_iteration(c):
@@ -35,7 +35,7 @@ def norms_iteration(c):
 
 
 def evac_on_vector(c, h):
-    return c < 13 or h == 0
+    return c < 13
 
 
 def tile_hyperbolicmlr_t_kernel(tc, x, a, p, out):
@@ -192,7 +192,8 @@ def tile_hyperbolicmlr_t_kernel(tc, x, a, p, out):
 
         def form_r(c):
             tt = work3.tile([P, SIZES[c] * P], F32, name="tt")
-            nc.gpsimd.tensor_scalar(out=tt[:], in0=T["ta", c][:], scalar1=3e38, scalar2=beta[:], op0=ALU.min, op1=ALU.max)
+            engine = nc.gpsimd if c < NCH - 2 else nc.vector
+            engine.tensor_scalar(out=tt[:], in0=T["ta", c][:], scalar1=3e38, scalar2=beta[:], op0=ALU.min, op1=ALU.max)
             T["tt", c] = tt
 
         def form_m(c):
@@ -236,7 +237,13 @@ def tile_hyperbolicmlr_t_kernel(tc, x, a, p, out):
         def turn(i):
             c = order[i]
             pool, nm = banks[i % len(banks)]
-            form_h(c)
+            if i >= 8:
+                if i == 8:
+                    form_h(c)
+                if i + 1 < NCH:
+                    form_h(order[i + 1])
+            else:
+                form_h(c)
             acc = pool.tile([P, SIZES[c], P], F32, name=nm)
             on_vector = i >= len(banks) and i % 2 == 1
             if on_vector:

@@ -27,11 +27,11 @@ TURNS = {-3: 1, -2: 1, -1: 2, 0: 2, 1: 2}
 
 
 def norms_on_vector(c):
-    return 0 if SIZES[c] < 4 else 2 if c < 6 else 1 if c % 2 == 0 else 0
+    return 0 if SIZES[c] < 4 else 2 if c < 6 else 1 if c % 4 == 0 else 0
 
 
 def norms_iteration(c):
-    return c - (5 if c < 6 else 6 if c < 9 else 7 if c < 13 else 8)
+    return c - (5 if c < 6 else 6 if c < 9 else 7 if c < NCH - 1 else 8)
 
 
 def evac_on_vector(c, h):
@@ -343,6 +343,8 @@ def tile_hyperbolicmlr_t_kernel(tc, x, a, p, out):
                 form_r(k)
             if ok(k + 2):
                 evac(k + 2, *halves(k + 2)[0])
+            if ok(k - 2) and not fresh:
+                square_z(k - 2)
             if ok(k):
                 form_m(k)
             if ok(k + 2) and len(halves(k + 2)) > 1:
@@ -376,7 +378,7 @@ def tile_hyperbolicmlr_t_kernel(tc, x, a, p, out):
                 setup_turn()
             if k == -2:
                 setup_rest()
-            if ok(k - 2):
+            if ok(k - 2) and fresh:
                 square_z(k - 2)
             for c in fresh:
                 if k > 0:

from contextlib import ExitStack

import concourse.mybir as mybir
from concourse.masks import make_identity

F32 = mybir.dt.float32
BF16 = mybir.dt.bfloat16
U32 = mybir.dt.uint32
U8 = mybir.dt.uint8
FP8X4 = mybir.dt.float8_e4m3fn_x4
ALU = mybir.AluOpType
ACT = mybir.ActivationFunctionType

B, D, C = 8192, 512, 128
P = 128
NT = B // P
KW = D // 2 // P
MAXN = 1.0 - 1e-5
FLOPS = 2 * B * D * 2 * C

SIZES = (1, 1, 2) + (4,) * 14 + (2, 2)
NCH = len(SIZES)
STARTS = tuple(sum(SIZES[:i]) for i in range(NCH))
PRE = 5
FAR = 16
TURNS = {-3: 1, -2: 1, -1: 2, 0: 2, 1: 2}


def norms_on_vector(c):
    return 0 if SIZES[c] < 4 else 2 if c < 6 else 1 if c % 4 == 0 else 0


def norms_iteration(c):
    return c - (5 if c < 6 else 6 if c < 9 else 7 if c < NCH - 1 else 8)


def evac_on_vector(c, h):
    return c < 13


def tile_hyperbolicmlr_t_kernel(tc, x, a, p, out):
    nc = tc.nc
    assert sum(SIZES) == NT
    xv = x.rearrange("(q g) k -> q g k", g=NT)
    ov = out.rearrange("(q g) c -> q g c", g=NT)
    with ExitStack() as ctx:
        const = ctx.enter_context(tc.tile_pool(name="const", bufs=1))
        keep = ctx.enter_context(tc.tile_pool(name="keep", bufs=1))
        xin = ctx.enter_context(tc.tile_pool(name="xin", bufs=9))
        small = ctx.enter_context(tc.tile_pool(name="small", bufs=12))
        work = ctx.enter_context(tc.tile_pool(name="work", bufs=2))
        work3 = ctx.enter_context(tc.tile_pool(name="work3", bufs=3))
        work4 = ctx.enter_context(tc.tile_pool(name="work4", bufs=4))
        stage = ctx.enter_context(tc.tile_pool(name="stage", bufs=8))
        ps_t = ctx.enter_context(tc.psum_pool(name="ps_t", bufs=3))
        ps_u = ctx.enter_context(tc.psum_pool(name="ps_u", bufs=2))
        ps_v = ctx.enter_context(tc.psum_pool(name="ps_v", bufs=2))
        ps_s = ctx.enter_context(tc.psum_pool(name="ps_s", bufs=1))
        ctx.enter_context(tc.manual_schedule())

        T = {}

        def ok(c):
            return 0 <= c < NCH

        def load(c):
            n = SIZES[c]
            xr = xin.tile([P, n, D], BF16, name="xr")
            nc.sync.dma_start(out=xr[:], in_=xv[:, STARTS[c]:STARTS[c] + n, :])
            T["xr", c] = xr

        def norms_v(c):
            n = SIZES[c]
            T["n2", c] = small.tile([P, n], F32, name="n2")
            for j in range(norms_on_vector(c)):
                xj = T["xr", c][:, j, :]
                junk = work.tile([P, D], BF16, name="junk_v")
                nc.vector.scalar_tensor_tensor(out=junk[:], in0=xj, scalar=1.0, in1=xj, op0=ALU.mult, op1=ALU.mult, accum_out=T["n2", c][:, j:j + 1])

        def norms_s(c, part, parts):
            first = norms_on_vector(c)
            tiles = range(first, SIZES[c])
            for j in tiles[part * len(tiles) // parts:(part + 1) * len(tiles) // parts]:
                junk = work.tile([P, D], BF16, name="junk_s")
                nc.scalar.activation(out=junk[:], in_=T["xr", c][:, j, :], func=ACT.Square, accum_out=T["n2", c][:, j:j + 1])

        def inv_norm(c):
            rn = small.tile([P, SIZES[c]], F32, name="rn")
            nc.scalar.activation(out=rn[:], in_=T["n2", c][:], func=ACT.Abs_reciprocal_sqrt)
            T["rn", c] = rn

        def plus_one(c):
            n = SIZES[c]
            if STARTS[c] < FAR:
                near = small.tile([P, n], F32, name="s1")
                s1 = near[:]
            else:
                s1 = far_in[STARTS[c] // FAR][:, STARTS[c] % FAR:STARTS[c] % FAR + n]
            nc.gpsimd.tensor_scalar(out=s1, in0=T["n2", c][:], scalar1=MAXN * MAXN, scalar2=1.0, op0=ALU.min, op1=ALU.add)
            T["s1", c] = s1

        def factor(c):
            sc = small.tile([P, SIZES[c]], F32, name="sc")
            nc.gpsimd.tensor_scalar(out=sc[:], in0=T["rn", c][:], scalar1=MAXN, scalar2=1.0, op0=ALU.mult, op1=ALU.min)
            T["sc", c] = sc

        def halves(c):
            n = SIZES[c]
            return [(h, min(2, n - 2 * h)) for h in range((n + 1) // 2)]

        def scale(c, h, m):
            if h == 0:
                T["xs", c] = work.tile([P, SIZES[c], D], BF16, name="xs")
            for j in range(2 * h, 2 * h + m):
                nc.vector.tensor_scalar(out=T["xs", c][:, j, :], in0=T["xr", c][:, j, :], scalar1=T["sc", c][:, j:j + 1], scalar2=None, op0=ALU.mult)

        def transp(c, h, m):
            pt = ps_t.tile([P, m, KW, P], F32, name="pt")
            for jj in range(m):
                words = T["xs", c][:, 2 * h + jj, :].bitcast(F32)
                for w in range(KW):
                    nc.tensor.transpose(pt[:, jj, w, :], words[:, w * P:(w + 1) * P], ident[:])
            T["pt", c, h] = pt

        def evac(c, h, m):
            if h == 0:
                T["gx", c] = work3.tile([P, SIZES[c] * P * 4], BF16, name="gx", align_bytes=64)
            dst = T["gx", c][:].bitcast(F32).rearrange("k (j r w) -> k j r w", r=P, w=KW)[:, 2 * h:2 * h + m, :, :]
            src = T["pt", c, h][:].rearrange("k j w r -> k j r w")
            if evac_on_vector(c, h):
                nc.vector.tensor_copy(out=dst, in_=src)
            else:
                nc.scalar.copy(out=dst, in_=src)

        def quant(c):
            n = SIZES[c]
            codes = work.tile([P, n * P], U32, name="codes", align_bytes=64)
            scales = work.tile([P, n * P], U8, name="scales", align_bytes=64)
            nc.vector.quantize_mx(out=codes[:].bitcast(FP8X4), scales=scales[:], in_=T["gx", c][:])
            T["codes", c] = codes
            T["scales", c] = scales

        def mx(c):
            n = SIZES[c]
            for i, (nm, pool) in enumerate((("pu", ps_u), ("pv", ps_v))):
                acc = pool.tile([P, n * P], F32, name=nm)
                nc.tensor.matmul_mx(
                    out=acc[:],
                    lhsT=w_codes[:, i * P:(i + 1) * P].bitcast(FP8X4),
                    lhsT_scale=w_scales[:, i * P:(i + 1) * P],
                    rhs=T["codes", c][:].bitcast(FP8X4),
                    rhs_scale=T["scales", c][:],
                    start=True,
                    stop=True,
                )
                T[nm, c] = acc

        def spread(c):
            n = SIZES[c]
            pb = ps_s.tile([P, n, P], F32, name="pb")
            for j in range(n):
                nc.tensor.transpose(pb[:, j, :], T["s1", c][:, j:j + 1].to_broadcast([P, P]), ident[:])
            T["pb", c] = pb

        def copy_s1(c):
            sb = work4.tile([P, SIZES[c] * P], F32, name="sb")
            nc.scalar.copy(out=sb[:], in_=T["pb", c][:].rearrange("k j r -> k (j r)"))
            T["sb", c] = sb[:]

        def turn_far(g):
            pb = ps_s.tile([P, P], F32, name="pb")
            nc.tensor.transpose(pb[:], far_in[g][:], ident[:])
            T["far", g] = pb

        def send_far(g):
            pb = T["far", g]
            rows = work.tile([P, P], F32, name="rows")
            nc.scalar.copy(out=rows[:], in_=pb[:])
            rest = out[g * FAR:(g + 1) * FAR, :]
            nc.sync.dma_start(out=rest, in_=rows[0:FAR, :])
            sb = keep.tile([P, FAR * P], F32, name="far%d" % g)
            nc.sync.dma_start(out=sb[:], in_=rest.rearrange("j r -> (j r)").partition_broadcast(P))
            for c in range(NCH):
                if STARTS[c] // FAR == g:
                    o = STARTS[c] % FAR
                    T["sb", c] = sb[:, o * P:(o + SIZES[c]) * P]

        def form_a(c):
            ta = work.tile([P, SIZES[c] * P], F32, name="ta")
            nc.vector.scalar_tensor_tensor(out=ta[:], in0=T["pu", c][:], scalar=-2.0, in1=T["sb", c], op0=ALU.mult, op1=ALU.add)
            T["ta", c] = ta

        def form_r(c):
            tt = work3.tile([P, SIZES[c] * P], F32, name="tt")
            engine = nc.gpsimd if c < NCH - 2 else nc.vector
            engine.tensor_scalar(out=tt[:], in0=T["ta", c][:], scalar1=3e38, scalar2=beta[:], op0=ALU.min, op1=ALU.max)
            T["tt", c] = tt

        def form_m(c):
            tm = keep.tile([P, SIZES[c] * P], F32, name="tm%d" % c)
            nc.vector.scalar_tensor_tensor(out=tm[:], in0=T["ta", c][:], scalar=fcol[:], in1=T["pv", c][:], op0=ALU.mult, op1=ALU.add)
            T["tm", c] = tm

        def form_t(c):
            tt = T["tt", c]
            nc.vector.scalar_tensor_tensor(out=tt[:], in0=T["sb", c], scalar=nhb[:], in1=tt[:], op0=ALU.mult, op1=ALU.add)

        def square_t(c):
            tt = T["tt", c]
            nc.scalar.activation(out=tt[:], in_=tt[:], func=ACT.Square)

        def inv_t(c):
            tt = T["tt", c]
            nc.scalar.activation(out=tt[:], in_=tt[:], func=ACT.Abs_reciprocal_sqrt)

        def form_z(c):
            tm = T["tm", c]
            nc.vector.scalar_tensor_tensor(out=tm[:], in0=tm[:], scalar=ecol[:], in1=T["tt", c][:], op0=ALU.mult, op1=ALU.mult)

        def square_z(c):
            sq = keep.tile([P, SIZES[c] * P], F32, name="sq%d" % c)
            nc.scalar.activation(out=sq[:], in_=T["tm", c][:], func=ACT.Square)
            T["sq", c] = sq

        def inv_h(c):
            tg = keep.tile([P, SIZES[c] * P], F32, name="tg%d" % c)
            nc.scalar.activation(out=tg[:], in_=T["sq", c][:], func=ACT.Abs_reciprocal_sqrt, bias=one1[:])
            T["tg", c] = tg

        def form_h(c):
            sq = T["sq", c]
            nc.vector.scalar_tensor_tensor(out=sq[:], in0=sq[:], scalar=1.0, in1=T["tg", c][:], op0=ALU.add, op1=ALU.mult)

        order = list(range(3, NCH)) + [2, 1, 0]
        banks = ((ps_s, "pb"), (ps_t, "pt"), (ps_t, "pt"), (ps_t, "pt"), (ps_u, "pu"), (ps_v, "pv"), (ps_u, "pu"), (ps_v, "pv"))

        def turn(i):
            c = order[i]
            pool, nm = banks[i % len(banks)]
            if i >= 8:
                if i == 8:
                    form_h(c)
                if i + 1 < NCH:
                    form_h(order[i + 1])
            else:
                form_h(c)
            acc = pool.tile([P, SIZES[c], P], F32, name=nm)
            on_vector = i >= len(banks) and i % 2 == 1
            if on_vector:
                nc.vector.tensor_tensor(out=T["sq", c][:], in0=T["sq", c][:], in1=T["tm", c][:], op=ALU.add)
            for j in range(SIZES[c]):
                cols = slice(j * P, (j + 1) * P)
                if on_vector:
                    nc.tensor.transpose(acc[:, j, :], T["sq", c][:, cols], ident[:])
                    continue
                nc.tensor.matmul(acc[:, j, :], lhsT=T["tm", c][:, cols], rhs=ident[:], start=True, stop=False, is_transpose=True)
                nc.tensor.matmul(acc[:, j, :], lhsT=T["sq", c][:, cols], rhs=ident[:], start=False, stop=True, is_transpose=True)
            T["acc", c] = acc

        load(0)
        pw = const.tile([P, D], BF16)
        aw = const.tile([P, D], BF16)
        nc.sync.dma_start(out=pw[:], in_=p)
        nc.sync.dma_start(out=aw[:], in_=a)
        for c in range(1, PRE):
            load(c)
        one1 = const.tile([P, 1], F32)
        nc.vector.memset(one1[:], 1.0)
        warm = const.tile([P, 1], F32)
        nc.scalar.activation(out=warm[:], in_=one1[:], func=ACT.Abs_reciprocal_sqrt)
        ident = const.tile([P, P], F32)
        make_identity(nc, ident[:])

        beta = const.tile([P, 1], F32)
        nhb = const.tile([P, 1], F32)
        fcol = const.tile([P, 1], F32)
        ecol = const.tile([P, 1], F32)
        far_in = {}
        for g in range(1, NT // FAR):
            far_in[g] = const.tile([P, P], F32, name="far_in%d" % g)
            nc.gpsimd.memset(far_in[g][:], 0.0)
        gw = const.tile([P, 2 * P * 4], BF16, align_bytes=64)
        sums = const.tile([P, 3], F32)
        ran = const.tile([P, 1], F32)
        w_codes = const.tile([P, 2 * P], U32, align_bytes=64)
        w_scales = const.tile([P, 2 * P], U8, align_bytes=64)

        def setup_sums():
            for s0, s1, i in ((pw, pw, 0), (aw, aw, 1), (pw, aw, 2)):
                junk_w = work.tile([P, D], BF16, name="junk_v")
                nc.vector.scalar_tensor_tensor(out=junk_w[:], in0=s0[:], scalar=1.0, in1=s1[:], op0=ALU.mult, op1=ALU.mult, accum_out=sums[:, i:i + 1])
            nc.scalar.activation(out=ran[:], in_=sums[:, 1:2], func=ACT.Abs_reciprocal_sqrt)

        def setup_turn():
            pwt = ps_t.tile([P, 2, KW, P], F32, name="pt")
            for i, src in enumerate((pw, aw)):
                words = src[:].bitcast(F32)
                for w in range(KW):
                    nc.tensor.transpose(pwt[:, i, w, :], words[:, w * P:(w + 1) * P], ident[:])
            nc.scalar.copy(out=gw[:].bitcast(F32).rearrange("k (i c w) -> k i c w", i=2, w=KW), in_=pwt[:].rearrange("k i w c -> k i c w"))

        def setup_rest():
            nc.vector.tensor_scalar(out=beta[:], in0=sums[:, 0:1], scalar1=-1.0, scalar2=1.0, op0=ALU.mult, op1=ALU.add)
            safe = const.tile([P, 1], F32)
            nc.vector.tensor_scalar(out=safe[:], in0=beta[:], scalar1=0.0, scalar2=1e-20, op0=ALU.is_equal, op1=ALU.mult)
            nc.vector.tensor_tensor(out=safe[:], in0=safe[:], in1=beta[:], op=ALU.add)
            rb = const.tile([P, 1], F32)
            nc.vector.reciprocal(out=rb[:], in_=safe[:])
            nc.vector.tensor_scalar(out=nhb[:], in0=beta[:], scalar1=-0.5, scalar2=None, op0=ALU.mult)
            nc.vector.tensor_scalar(out=fcol[:], in0=sums[:, 2:3], scalar1=rb[:], scalar2=-1.0, op0=ALU.mult, op1=ALU.mult)
            nc.vector.tensor_scalar(out=ecol[:], in0=safe[:], scalar1=ran[:], scalar2=-1.0, op0=ALU.mult, op1=ALU.mult)
            nc.vector.quantize_mx(out=w_codes[:].bitcast(FP8X4), scales=w_scales[:], in_=gw[:])

        nturn = 0
        for k in range(-5, NCH + 3):
            if ok(k + 5 + PRE):
                load(k + 5 + PRE)
            first = halves(k + 3)[0] if ok(k + 3) else None
            second = halves(k + 3)[1] if ok(k + 3) and len(halves(k + 3)) > 1 else None
            fresh = [c for c in range(NCH) if norms_iteration(c) == k]
            if ok(k + 4) and k <= 0:
                inv_norm(k + 4)
                factor(k + 4)
            for c in fresh:
                norms_v(c)
                if k <= 0:
                    norms_s(c, 0, 1)
            groups = []
            for c in range(NCH):
                if norms_iteration(c) == k - 1:
                    plus_one(c)
                    if STARTS[c] >= FAR and (STARTS[c] + SIZES[c]) % FAR == 0:
                        groups.append(STARTS[c] // FAR)
            if ok(k + 2) and STARTS[k + 2] < FAR:
                spread(k + 2)
            if ok(k + 1):
                quant(k + 1)
                mx(k + 1)
            if ok(k - 1):
                square_t(k - 1)
            if ok(k):
                form_a(k)
                form_r(k)
            if ok(k + 2):
                evac(k + 2, *halves(k + 2)[0])
            if ok(k - 2) and not fresh:
                square_z(k - 2)
            if ok(k):
                form_m(k)
            if ok(k + 2) and len(halves(k + 2)) > 1:
                evac(k + 2, *halves(k + 2)[1])
            for c in fresh:
                if k > 0:
                    norms_s(c, 0, 4)
            if ok(k - 1):
                inv_t(k - 1)
            for c in fresh:
                if k > 0:
                    norms_s(c, 1, 4)
            if ok(k + 4) and k > 0:
                inv_norm(k + 4)
                factor(k + 4)
            if first:
                scale(k + 3, *first)
                transp(k + 3, *first)
            if ok(k + 2) and STARTS[k + 2] < FAR:
                copy_s1(k + 2)
            if second:
                scale(k + 3, *second)
                transp(k + 3, *second)
            for g in groups:
                turn_far(g)
            if ok(k):
                form_t(k)
            if k == -4:
                setup_sums()
            if k == -3:
                setup_turn()
            if k == -2:
                setup_rest()
            if ok(k - 2) and fresh:
                square_z(k - 2)
            for c in fresh:
                if k > 0:
                    norms_s(c, 2, 4)
            if ok(k - 2):
                inv_h(k - 2)
            for c in fresh:
                if k > 0:
                    norms_s(c, 3, 4)
            for g in groups:
                send_far(g)
            if ok(k - 1):
                form_z(k - 1)
            for i in range(TURNS.get(k - NCH, 0)):
                turn(nturn)
                nturn += 1

        for i, c in enumerate(order):
            n = SIZES[c]
            if i >= nturn:
                turn(i)
            res = stage.tile([P, n, P], F32, name="res")
            nc.scalar.activation(out=res[:], in_=T["acc", c][:], func=ACT.Ln)
            nc.sync.dma_start(out=ov[:, STARTS[c]:STARTS[c] + n, :], in_=res[:])
